import numpy as np
import ml_dtypes


def mxq(x, axis, fmt="e4m3"):
    dtype, down = {"e4m3": (ml_dtypes.float8_e4m3fn, 7), "e5m2": (ml_dtypes.float8_e5m2, 14)}[fmt]
    v = np.moveaxis(np.asarray(x, np.float32).astype(ml_dtypes.bfloat16).astype(np.float64), axis, -1)
    blocks = v.reshape(v.shape[:-1] + (-1, 32))
    amax = np.abs(blocks).max(-1, keepdims=True)
    byte = np.maximum(np.where(amax > 0, np.frexp(amax)[1] - 1 + 127, 0) - down, 1)
    scale = np.exp2(byte - 127.0)
    codes = (blocks / scale).astype(np.float32).astype(dtype).astype(np.float64)
    return np.moveaxis((codes * scale).reshape(v.shape), -1, axis)


WIDE = False


def mx_kscale(k):
    if not WIDE:
        return np.ones(k)
    levels = np.array([10, -10, 5, -5, 0])
    if k % 512:
        return np.exp2(np.random.permutation(np.resize(levels, k // 32))).repeat(32)
    a = np.empty((k // 512, 16))
    for p in range(k // 512):
        a[p, :8] = np.random.permutation(np.resize(levels, 8))
        for g in range(8):
            far = levels[np.abs(levels - a[p, g]) >= 10]
            a[p, g + 8] = far[np.random.randint(len(far))]
    return np.exp2(a.ravel()).repeat(32)


BF16 = ml_dtypes.bfloat16


def bf(x):
    return np.asarray(x, np.float32).astype(BF16)


def f64(x):
    return np.asarray(x).astype(np.float64)


B, S, E, H, KV, DH = 1, 512, 2048, 16, 4, 128
THETA = 10000.0


def rope(x):
    b, s, h, hd = x.shape
    half = hd // 2
    inv_freq = 1.0 / THETA ** (f64(np.arange(0, half, 2)) / half)
    pos = np.broadcast_to(f64(np.arange(s))[None, :], (b, s))
    freqs = pos[:, :, None] * inv_freq[None, None, :]
    cos = np.cos(freqs)[:, :, None, :]
    sin = np.sin(freqs)[:, :, None, :]
    pairs = x[..., :half].reshape(b, s, h, half // 2, 2)
    x0, x1 = pairs[..., 0], pairs[..., 1]
    rot = np.stack([x0 * cos - x1 * sin, x0 * sin + x1 * cos], axis=-1).reshape(b, s, h, half)
    return np.concatenate([rot, x[..., half:]], axis=-1)


def draw0():
    s = mx_kscale(E)
    return {"hidden_states": bf(np.random.standard_normal((B, S, E)) * s),
            "Wq": bf(np.random.standard_normal((E, H * DH)) * 1.25 / np.sqrt(E) / s[:, None]),
            "Wk": bf(np.random.standard_normal((E, KV * DH)) * 1.25 / np.sqrt(E) / s[:, None]),
            "Wv": bf(np.random.standard_normal((E, KV * DH)) * 1.25 / np.sqrt(E) / s[:, None])}


def core(hidden_states, Wq, Wk, Wv):
    xq = mxq(f64(hidden_states), 2, "e4m3")
    q = (xq @ mxq(f64(Wq), 0, "e4m3")).reshape(B, S, H, DH)
    k = (xq @ mxq(f64(Wk), 0, "e4m3")).reshape(B, S, KV, DH)
    v = (xq @ mxq(f64(Wv), 0, "e4m3")).reshape(B, S, KV, DH)
    return rope(q), rope(k), v


def e4m3fn_bytes(y):
    return np.clip(np.asarray(y, np.float64), -448.0, 448.0).astype(np.float32).astype(ml_dtypes.float8_e4m3fn).view(np.uint8)


def e4m3fn_values(b):
    return np.asarray(b, np.uint8).view(ml_dtypes.float8_e4m3fn).astype(np.float64)


def setup_inputs():
    d = draw0()
    x0 = np.asarray(d['Wq']).astype(np.float64)
    s = (np.max(np.abs(x0), axis=(1,), keepdims=True) / 448.0).astype(np.float32)
    out = {}
    for k, v in d.items():
        if k == 'Wq':
            out['Wq_bytes'] = e4m3fn_bytes(x0 / s.astype(np.float64))
            out['Wq_scale'] = s
        else:
            out[k] = v
    return out


def reference(hidden_states, Wq_bytes, Wq_scale, Wk, Wv):
    return core(hidden_states, e4m3fn_values(Wq_bytes) * Wq_scale.astype(np.float64), Wk, Wv)

@@ -1,0 +1,302 @@
+import math
+from contextlib import ExitStack
+
+import concourse.mybir as mybir
+from concourse.masks import make_identity
+
+FLOPS = 2 * 512 * 2048 * 3072
+
+F32 = mybir.dt.float32
+BF16 = mybir.dt.bfloat16
+U32 = mybir.dt.uint32
+U8 = mybir.dt.uint8
+I32 = mybir.dt.int32
+FP8 = mybir.dt.float8_e4m3fn
+FP8X4 = mybir.dt.float8_e4m3fn_x4
+ALU = mybir.AluOpType
+ACT = mybir.ActivationFunctionType
+
+P = 128
+PACK = 4
+TT = 4
+G = 4
+PAIRS = 32
+FREQ_STEP = 10000.0 ** (-1.0 / 32.0)
+TWO_PI_HI = 6.28125
+TWO_PI_LO = 2.0 * math.pi - TWO_PI_HI
+
+SCALAR_Q_UNITS = ((1, 1, 1), (1, 3, 1))
+
+
+def tile_diffucoderattention_pa_kernel(tc, hidden_states, Wq_bytes, Wq_scale, Wk, Wv, out_0, out_1, out_2):
+    nc = tc.nc
+    x_rows = hidden_states.rearrange("o s k -> (o s) k")
+    q_out = out_0.rearrange("o s h d -> (o s) (h d)")
+    k_out = out_1.rearrange("o s h d -> (o s) (h d)")
+    v_out = out_2.rearrange("o s h d -> (o s) (h d)")
+    wq_view = Wq_bytes.rearrange("(g p t) n -> g p t n", p=P, t=PACK)
+    wk_view = Wk.rearrange("(g p t) n -> g p t n", p=P, t=PACK)
+    wv_view = Wv.rearrange("(g p t) n -> g p t n", p=P, t=PACK)
+
+    with ExitStack() as ctx:
+        const = ctx.enter_context(tc.tile_pool(name="const", bufs=1))
+        raw = ctx.enter_context(tc.tile_pool(name="raw", bufs=1))
+        keep = ctx.enter_context(tc.tile_pool(name="keep", bufs=1))
+        xy = ctx.enter_context(tc.tile_pool(name="xy", bufs=6))
+        widep = ctx.enter_context(tc.tile_pool(name="widep", bufs=3))
+        ilp = ctx.enter_context(tc.tile_pool(name="ilp", bufs=4))
+        zp = ctx.enter_context(tc.tile_pool(name="zp", bufs=3))
+        psum = ctx.enter_context(tc.psum_pool(name="psum", bufs=8))
+
+        scl = const.tile([P, G * PACK], F32, name="scl")
+        nc.sync.dma_start(
+            out=scl[:].rearrange("p (g t) -> p g t", t=PACK),
+            in_=Wq_scale.rearrange("(g p t) o -> p g (t o)", p=P, t=PACK),
+        )
+        wq_bytes = {}
+        wk_raw = {}
+        wv_raw = {}
+        x_sb = {}
+
+        def load_q(j, g):
+            tl = raw.tile([P, PACK, 1024], U8, name="wq_bytes_%d_%d" % (j, g))
+            nc.sync.dma_start(out=tl[:], in_=wq_view[g][:, :, j * 1024 : (j + 1) * 1024])
+            wq_bytes[(j, g)] = tl
+
+        def load_k(g):
+            tl = raw.tile([P, PACK, 512], BF16, name="wk_raw_%d" % g)
+            nc.sync.dma_start(out=tl[:], in_=wk_view[g])
+            wk_raw[g] = tl
+
+        def load_v(g):
+            tl = raw.tile([P, PACK, 512], BF16, name="wv_raw_%d" % g)
+            nc.sync.dma_start(out=tl[:], in_=wv_view[g])
+            wv_raw[g] = tl
+
+        def load_x(tt):
+            tl = xy.tile([P, 2048], BF16, name="x_sb_%d" % tt, tag="xy")
+            nc.sync.dma_start(out=tl[:], in_=x_rows[tt * P : (tt + 1) * P, :])
+            x_sb[tt] = tl
+
+        load_q(0, 0)
+        load_k(0)
+        load_k(1)
+        load_q(0, 1)
+        load_k(2)
+        load_k(3)
+        load_q(0, 2)
+        load_x(0)
+        load_x(1)
+        load_q(0, 3)
+        load_x(2)
+        load_x(3)
+        for g in range(G):
+            load_q(1, g)
+        for g in range(G):
+            load_v(g)
+
+        warm = const.tile([P, 2], F32, name="warm")
+        nc.vector.memset(warm[:], 0.0)
+        nc.scalar.activation(out=warm[:, 1:2], in_=warm[:, 0:1], func=ACT.Sin)
+
+        ident = const.tile([P, P], F32, name="ident")
+        make_identity(nc, ident[:])
+
+        pos = const.tile([P, TT], F32, name="pos")
+        nc.gpsimd.iota(pos[:], pattern=[[P, TT]], base=0, channel_multiplier=1, allow_small_or_imprecise_dtypes=True)
+        ang = const.tile([P, TT, PAIRS], F32, name="ang")
+        nc.vector.tensor_copy(out=ang[:, :, 0:1], in_=pos[:].unsqueeze(2))
+        for w in (1, 2, 4, 8, 16):
+            nc.vector.tensor_scalar(
+                out=ang[:, :, w : 2 * w], in0=ang[:, :, 0:w], scalar1=FREQ_STEP**w, scalar2=None, op0=ALU.mult
+            )
+        ang_flat = ang[:].rearrange("p t i -> p (t i)")
+        turns_i = const.tile([P, TT * PAIRS], I32, name="turns_i")
+        nc.vector.tensor_scalar(out=turns_i[:], in0=ang_flat, scalar1=1.0 / (2.0 * math.pi), scalar2=None, op0=ALU.mult)
+        turns = const.tile([P, TT * PAIRS], F32, name="turns")
+        nc.vector.tensor_copy(out=turns[:], in_=turns_i[:])
+        red1 = const.tile([P, TT * PAIRS], F32, name="red1")
+        nc.vector.scalar_tensor_tensor(out=red1[:], in0=turns[:], scalar=-TWO_PI_HI, in1=ang_flat, op0=ALU.mult, op1=ALU.add)
+        red2 = const.tile([P, TT * PAIRS], F32, name="red2")
+        nc.vector.scalar_tensor_tensor(out=red2[:], in0=turns[:], scalar=-TWO_PI_LO, in1=red1[:], op0=ALU.mult, op1=ALU.add)
+        wrap = const.tile([P, TT * PAIRS], F32, name="wrap")
+        nc.vector.tensor_scalar(out=wrap[:], in0=red2[:], scalar1=math.pi, scalar2=-2.0 * math.pi, op0=ALU.is_gt, op1=ALU.mult)
+        red = const.tile([P, TT * PAIRS], F32, name="red")
+        nc.vector.tensor_tensor(out=red[:], in0=red2[:], in1=wrap[:], op=ALU.add)
+        mag = const.tile([P, TT * PAIRS], F32, name="mag")
+        nc.vector.scalar_tensor_tensor(out=mag[:], in0=red[:], scalar=-1.0, in1=red[:], op0=ALU.mult, op1=ALU.max)
+        red3 = red[:].rearrange("p (t i) -> p t i", i=PAIRS)
+        mag3 = mag[:].rearrange("p (t i) -> p t i", i=PAIRS)
+        tab = const.tile([P, TT, 2, PAIRS, 2], F32, name="tab")
+        nc.scalar.activation(out=tab[:, :, 0, :, 1], in_=red3, func=ACT.Sin)
+        nc.scalar.activation(out=tab[:, :, 1, :, 0], in_=red3, func=ACT.Sin, scale=-1.0)
+        nc.scalar.activation(out=tab[:, :, 0, :, 0], in_=mag3, func=ACT.Sin, scale=-1.0, bias=math.pi / 2.0)
+        nc.scalar.activation(out=tab[:, :, 1, :, 1], in_=mag3, func=ACT.Sin, scale=-1.0, bias=math.pi / 2.0)
+
+        xc = {}
+        xs = {}
+        for tt in range(TT):
+            xc[tt] = keep.tile([P, G * P], U32, name="xc_%d" % tt, align_bytes=64)
+            xs[tt] = keep.tile([P, G * P], U8, name="xs_%d" % tt, align_bytes=64)
+        qc = {}
+        qs = {}
+        for j in range(2):
+            qc[j] = keep.tile([P, 2, G, 512], U32, name="qc_%d" % j, align_bytes=64)
+            qs[j] = keep.tile([P, 2, G, 512], U8, name="qs_%d" % j, align_bytes=64)
+        kc = keep.tile([P, G, 512], U32, name="kc", align_bytes=64)
+        ks = keep.tile([P, G, 512], U8, name="ks", align_bytes=64)
+        vc = keep.tile([P, G, 512], U32, name="vc", align_bytes=64)
+        vs = keep.tile([P, G, 512], U8, name="vs", align_bytes=64)
+
+        def copy_on(eng, out, in_):
+            if eng == "v":
+                nc.vector.tensor_copy(out=out, in_=in_)
+            else:
+                nc.scalar.copy(out=out, in_=in_)
+
+        def quantize(il, codes, scales):
+            nc.vector.quantize_mx(out=codes.bitcast(FP8X4), scales=scales, in_=il[:])
+
+        wide = {}
+
+        def widen(j, g):
+            tl = widep.tile([P, PACK, 1024], BF16, name="wide", tag="wide")
+            for t in range(PACK):
+                nc.scalar.activation(
+                    out=tl[:, t, :],
+                    in_=wq_bytes[(j, g)][:, t, :].bitcast(FP8),
+                    func=ACT.Copy,
+                    scale=scl[:, PACK * g + t : PACK * g + t + 1],
+                )
+            wide[(j, g)] = tl
+
+        def il_q(j, g, half):
+            il = ilp.tile([P, 2048], BF16, name="il", tag="il", align_bytes=64)
+            src = wide[(j, g)][:].rearrange("p t (h f) -> p h f t", f=128)[:, :, half * 64 : (half + 1) * 64, :]
+            dst = il[:].rearrange("p (h f t) -> p h f t", h=8, t=PACK)
+            copy_on("s" if (j, g, half) in SCALAR_Q_UNITS else "v", dst, src)
+            return il
+
+        def il_k(g):
+            il = ilp.tile([P, 2048], BF16, name="il", tag="il", align_bytes=64)
+            for half in range(2):
+                src = wk_raw[g][:].rearrange("p t (h f) -> p h f t", f=128)[:, :, half * 64 : (half + 1) * 64, :]
+                dst = il[:, half * 1024 : (half + 1) * 1024].rearrange("p (h f t) -> p h f t", h=4, t=PACK)
+                copy_on("v", dst, src)
+            return il
+
+        def il_v(g):
+            il = ilp.tile([P, 2048], BF16, name="il", tag="il", align_bytes=64)
+            copy_on("s", il[:].rearrange("p (n t) -> p n t", t=PACK), wv_raw[g][:].rearrange("p t n -> p n t"))
+            return il
+
+        def matmuls(tt, codes, scales, n):
+            acc = psum.tile([P, 512], F32, name="acc", tag="bank")
+            for g in range(G):
+                nc.tensor.matmul_mx(
+                    out=acc[:, 0:n],
+                    lhsT=xc[tt][:, g * P : (g + 1) * P].bitcast(FP8X4),
+                    lhsT_scale=xs[tt][:, g * P : (g + 1) * P],
+                    rhs=codes(g).bitcast(FP8X4),
+                    rhs_scale=scales(g),
+                    start=(g == 0),
+                    stop=(g == G - 1),
+                )
+            return acc
+
+        def rope(tt, acc, heads, y):
+            n = heads * 64
+            z = zp.tile([P, 2, 512], F32, name="z", tag="z")
+            shape = [P, heads, PAIRS, 2]
+            for r in range(2):
+                nc.vector.tensor_tensor(
+                    out=z[:, r, 0:n].rearrange("p (h i e) -> p h i e", h=heads, e=2),
+                    in0=acc[:, 0:n].rearrange("p (h i e) -> p h i e", h=heads, e=2)[:, :, :, r : r + 1].to_broadcast(shape),
+                    in1=tab[:, tt, r, :, :].unsqueeze(1).to_broadcast(shape),
+                    op=ALU.mult,
+                )
+            nc.vector.tensor_tensor(
+                out=y[:].rearrange("p (h f) -> p h f", f=128)[:, :, 0:64],
+                in0=z[:, 0, 0:n].rearrange("p (h f) -> p h f", f=64),
+                in1=z[:, 1, 0:n].rearrange("p (h f) -> p h f", f=64),
+                op=ALU.add,
+            )
+
+        def plain(acc, heads, y):
+            nc.scalar.copy(
+                out=y[:].rearrange("p (h f) -> p h f", f=128)[:, :, 64:128],
+                in_=acc[:, 0 : heads * 64].rearrange("p (h f) -> p h f", f=64),
+            )
+
+        widen(0, 0)
+        widen(0, 1)
+
+        prev = None
+        for g in range(G):
+            il = il_k(g)
+            if prev is not None:
+                quantize(prev[0], kc[:, prev[1], :], ks[:, prev[1], :])
+            prev = (il, g)
+        quantize(prev[0], kc[:, prev[1], :], ks[:, prev[1], :])
+
+        for tt in range(TT):
+            words = x_sb[tt][:].bitcast(F32)
+            xg = ilp.tile([P, 2048], BF16, name="xg", tag="il", align_bytes=64)
+            for gp in range(2):
+                xt = psum.tile([P, 512], F32, name="xt", tag="bank")
+                for gl in range(2):
+                    g = 2 * gp + gl
+                    for u in range(2):
+                        nc.tensor.transpose(
+                            xt[:, (2 * gl + u) * P : (2 * gl + u + 1) * P],
+                            words[:, 256 * g + u : 256 * (g + 1) : 2],
+                            ident[:],
+                        )
+                copy_on(
+                    "v" if gp == 0 else "s",
+                    xg[:].bitcast(F32).rearrange("p (g r u) -> p g r u", g=G, u=2)[:, 2 * gp : 2 * gp + 2, :, :],
+                    xt[:].rearrange("p (g u r) -> p g r u", g=2, u=2),
+                )
+            nc.vector.quantize_mx(out=xc[tt][:].bitcast(FP8X4), scales=xs[tt][:], in_=xg[:])
+
+        for tt in range(TT):
+            y = xy.tile([P, 512], F32, name="y_k", tag="xy")
+            acc = matmuls(tt, lambda g: kc[:, g, 0:256], lambda g: ks[:, g, 0:256], 256)
+            rope(tt, acc, 4, y)
+            acc = matmuls(tt, lambda g: kc[:, g, 256:512], lambda g: ks[:, g, 256:512], 256)
+            plain(acc, 4, y)
+            nc.sync.dma_start(out=k_out[tt * P : (tt + 1) * P, :], in_=y[:])
+
+        for j in range(2):
+            prev = []
+            for g in range(G):
+                nxt = 4 * j + g + 2
+                if nxt < 8:
+                    widen(nxt // 4, nxt % 4)
+                cur = []
+                for half in range(2):
+                    cur.append((il_q(j, g, half), half, g))
+                for il, half, gg in prev:
+                    quantize(il, qc[j][:, half, gg, :], qs[j][:, half, gg, :])
+                prev = cur
+            for il, half, gg in prev:
+                quantize(il, qc[j][:, half, gg, :], qs[j][:, half, gg, :])
+
+            if j == 1:
+                for g in range(G):
+                    il = il_v(g)
+                    quantize(il, vc[:, g, :], vs[:, g, :])
+
+            for tt in range(TT):
+                y = xy.tile([P, 1024], F32, name="y_q", tag="xy")
+                acc = matmuls(tt, lambda g: qc[j][:, 0, g, :], lambda g: qs[j][:, 0, g, :], 512)
+                rope(tt, acc, 8, y)
+                acc = matmuls(tt, lambda g: qc[j][:, 1, g, :], lambda g: qs[j][:, 1, g, :], 512)
+                plain(acc, 8, y)
+                nc.sync.dma_start(out=q_out[tt * P : (tt + 1) * P, j * 1024 : (j + 1) * 1024], in_=y[:])
+
+        for tt in range(TT):
+            y = xy.tile([P, 512], F32, name="y_v", tag="xy")
+            acc = matmuls(tt, lambda g: vc[:, g, :], lambda g: vs[:, g, :], 512)
+            copy_on("s" if tt % 2 == 0 else "v", y[:], acc[:])
+            nc.sync.dma_start(out=v_out[tt * P : (tt + 1) * P, :], in_=y[:])

@@ -172,22 +172,22 @@ def tile_diffucoderattention_pa_kernel(tc, hidden_states, Wq_bytes, Wq_scale, Wk
 
         def il_q(j, g, half):
             il = ilp.tile([P, 2048], BF16, name="il", tag="il", align_bytes=64)
-            src = wide[(j, g)][:].rearrange("p t (h f) -> p h f t", f=128)[:, :, half * 64 : (half + 1) * 64, :]
-            dst = il[:].rearrange("p (h f t) -> p h f t", h=8, t=PACK)
+            src = wide[(j, g)][:].rearrange("p t (h c i) -> p h c t i", h=8, i=4)[:, :, half * 16 : (half + 1) * 16, :, :]
+            dst = il[:].rearrange("p (h c i t) -> p h c t i", h=8, i=4, t=PACK)
             copy_on("s" if (j, g, half) in SCALAR_Q_UNITS else "v", dst, src)
             return il
 
         def il_k(g):
             il = ilp.tile([P, 2048], BF16, name="il", tag="il", align_bytes=64)
             for half in range(2):
-                src = wk_raw[g][:].rearrange("p t (h f) -> p h f t", f=128)[:, :, half * 64 : (half + 1) * 64, :]
-                dst = il[:, half * 1024 : (half + 1) * 1024].rearrange("p (h f t) -> p h f t", h=4, t=PACK)
+                src = wk_raw[g][:].rearrange("p t (h c i) -> p h c t i", h=4, i=4)[:, :, half * 16 : (half + 1) * 16, :, :]
+                dst = il[:, half * 1024 : (half + 1) * 1024].rearrange("p (h c i t) -> p h c t i", h=4, i=4, t=PACK)
                 copy_on("v", dst, src)
             return il
 
         def il_v(g):
             il = ilp.tile([P, 2048], BF16, name="il", tag="il", align_bytes=64)
-            copy_on("s", il[:].rearrange("p (n t) -> p n t", t=PACK), wv_raw[g][:].rearrange("p t n -> p n t"))
+            copy_on("s", il[:].rearrange("p (c i t) -> p c t i", i=4, t=PACK), wv_raw[g][:].rearrange("p t (c i) -> p c t i", i=4))
             return il
 
         def matmuls(tt, codes, scales, n):

@@ -25,7 +25,7 @@ FREQ_STEP = 10000.0 ** (-1.0 / 32.0)
 TWO_PI_HI = 6.28125
 TWO_PI_LO = 2.0 * math.pi - TWO_PI_HI
 
-SCALAR_Q_UNITS = ((1, 1, 1), (1, 3, 1))
+TENSOR_Q_UNITS = ((0, 1), (0, 3), (1, 0), (1, 1), (1, 2))
 
 
 def tile_diffucoderattention_pa_kernel(tc, hidden_states, Wq_bytes, Wq_scale, Wk, Wv, out_0, out_1, out_2):
@@ -46,7 +46,7 @@ def tile_diffucoderattention_pa_kernel(tc, hidden_states, Wq_bytes, Wq_scale, Wk
         widep = ctx.enter_context(tc.tile_pool(name="widep", bufs=3))
         ilp = ctx.enter_context(tc.tile_pool(name="ilp", bufs=4))
         zp = ctx.enter_context(tc.tile_pool(name="zp", bufs=3))
-        psum = ctx.enter_context(tc.psum_pool(name="psum", bufs=8))
+        psum = ctx.enter_context(tc.psum_pool(name="psum", bufs=6))
 
         scl = const.tile([P, G * PACK], F32, name="scl")
         nc.sync.dma_start(
@@ -90,10 +90,12 @@ def tile_diffucoderattention_pa_kernel(tc, hidden_states, Wq_bytes, Wq_scale, Wk
         load_q(0, 3)
         load_x(2)
         load_x(3)
-        for g in range(G):
-            load_q(1, g)
+        load_q(1, 0)
+        load_q(1, 1)
         for g in range(G):
             load_v(g)
+        load_q(1, 2)
+        load_q(1, 3)
 
         warm = const.tile([P, 2], F32, name="warm")
         nc.vector.memset(warm[:], 0.0)
@@ -101,6 +103,8 @@ def tile_diffucoderattention_pa_kernel(tc, hidden_states, Wq_bytes, Wq_scale, Wk
 
         ident = const.tile([P, P], F32, name="ident")
         make_identity(nc, ident[:])
+        ident_bf = const.tile([P, P], BF16, name="ident_bf")
+        make_identity(nc, ident_bf[:])
 
         pos = const.tile([P, TT], F32, name="pos")
         nc.gpsimd.iota(pos[:], pattern=[[P, TT]], base=0, channel_multiplier=1, allow_small_or_imprecise_dtypes=True)
@@ -174,8 +178,21 @@ def tile_diffucoderattention_pa_kernel(tc, hidden_states, Wq_bytes, Wq_scale, Wk
             il = ilp.tile([P, 2048], BF16, name="il", tag="il", align_bytes=64)
             src = wide[(j, g)][:].rearrange("p t (h c i) -> p h c t i", h=8, i=4)[:, :, half * 16 : (half + 1) * 16, :, :]
             dst = il[:].rearrange("p (h c i t) -> p h c t i", h=8, i=4, t=PACK)
-            copy_on("s" if (j, g, half) in SCALAR_Q_UNITS else "v", dst, src)
+            copy_on("v", dst, src)
             return il
+
+        def il_tensor(view):
+            il = ilp.tile([P, 2048], BF16, name="ilt", tag="ilt", bufs=3, align_bytes=64)
+            for b in range(2):
+                st = psum.tile([P, 1024], BF16, name="st", tag="stage", bufs=2)
+                for m in range(2):
+                    nc.tensor.matmul(out=st[:, m * 512 : (m + 1) * 512], lhsT=ident_bf[:], rhs=view(2 * b + m), start=True, stop=True)
+                nc.scalar.copy(out=il[:, b * 1024 : (b + 1) * 1024], in_=st[:])
+            return il
+
+        def il_q_tensor(j, g):
+            planes = wide[(j, g)][:].rearrange("p t (h f) -> p h f t", f=128)
+            return il_tensor(lambda m: planes[:, 2 * m : 2 * m + 2, 64:128, :])
 
         def il_k(g):
             il = ilp.tile([P, 2048], BF16, name="il", tag="il", align_bytes=64)
@@ -186,13 +203,11 @@ def tile_diffucoderattention_pa_kernel(tc, hidden_states, Wq_bytes, Wq_scale, Wk
             return il
 
         def il_v(g):
-            il = ilp.tile([P, 2048], BF16, name="il", tag="il", align_bytes=64)
-            copy_on("s", il[:].rearrange("p (c i t) -> p c t i", i=4, t=PACK), wv_raw[g][:].rearrange("p t (c i) -> p c t i", i=4))
-            return il
+            planes = wv_raw[g][:].rearrange("p t n -> p n t")
+            return il_tensor(lambda m: planes[:, m * P : (m + 1) * P, :])
 
-        def matmuls(tt, codes, scales, n):
-            acc = psum.tile([P, 512], F32, name="acc", tag="bank")
-            for g in range(G):
+        def one_pass(acc, tt, g, codes, scales, n):
+            if True:
                 nc.tensor.matmul_mx(
                     out=acc[:, 0:n],
                     lhsT=xc[tt][:, g * P : (g + 1) * P].bitcast(FP8X4),
@@ -202,9 +217,14 @@ def tile_diffucoderattention_pa_kernel(tc, hidden_states, Wq_bytes, Wq_scale, Wk
                     start=(g == 0),
                     stop=(g == G - 1),
                 )
+
+        def matmuls(tt, codes, scales, n):
+            acc = psum.tile([P, 512], F32, name="acc", tag="bank")
+            for g in range(G):
+                one_pass(acc, tt, g, codes, scales, n)
             return acc
 
-        def rope(tt, acc, heads, y):
+        def rope(tt, acc, heads, y, add_eng):
             n = heads * 64
             z = zp.tile([P, 2, 512], F32, name="z", tag="z")
             shape = [P, heads, PAIRS, 2]
@@ -215,33 +235,89 @@ def tile_diffucoderattention_pa_kernel(tc, hidden_states, Wq_bytes, Wq_scale, Wk
                     in1=tab[:, tt, r, :, :].unsqueeze(1).to_broadcast(shape),
                     op=ALU.mult,
                 )
-            nc.vector.tensor_tensor(
+            add_eng.tensor_tensor(
                 out=y[:].rearrange("p (h f) -> p h f", f=128)[:, :, 0:64],
                 in0=z[:, 0, 0:n].rearrange("p (h f) -> p h f", f=64),
                 in1=z[:, 1, 0:n].rearrange("p (h f) -> p h f", f=64),
                 op=ALU.add,
             )
 
-        def plain(acc, heads, y):
-            nc.scalar.copy(
-                out=y[:].rearrange("p (h f) -> p h f", f=128)[:, :, 64:128],
-                in_=acc[:, 0 : heads * 64].rearrange("p (h f) -> p h f", f=64),
+        def plain(acc, heads, y, eng):
+            copy_on(
+                eng,
+                y[:].rearrange("p (h f) -> p h f", f=128)[:, :, 64:128],
+                acc[:, 0 : heads * 64].rearrange("p (h f) -> p h f", f=64),
             )
+
+        ctx.enter_context(tc.manual_schedule(engines={mybir.EngineType.DVE, mybir.EngineType.Pool}))
+
+        pending = []
+        late = []
+        done = {"pending": 0, "late": 0}
+        rot1 = {"open": False, "ready": [], "acc": {}}
+
+        def rot1_passes():
+            if rot1["open"]:
+                for g in rot1["ready"]:
+                    for tt in range(TT):
+                        one_pass(rot1["acc"][tt], tt, g, lambda gg: qc[1][:, 0, gg, :], lambda gg: qs[1][:, 0, gg, :], 512)
+                rot1["ready"].clear()
+
+        def run(unit):
+            il, codes, scales, mark = unit
+            quantize(il, codes, scales)
+            if mark is not None:
+                rot1["ready"].append(mark)
+                rot1_passes()
+
+        def flush(keep):
+            while len(pending) - done["pending"] > keep:
+                run(pending[done["pending"]])
+                done["pending"] += 1
+
+        def flush_late():
+            while len(late) - done["late"] > 0:
+                run(late[done["late"]])
+                done["late"] += 1
+
+        def q_unit(j, g, half):
+            mark = g if (j == 1 and half == 0) else None
+            if half == 1 and (j, g) in TENSOR_Q_UNITS:
+                late.append((il_q_tensor(j, g), qc[j][:, half, g, :], qs[j][:, half, g, :], mark))
+            else:
+                pending.append((il_q(j, g, half), qc[j][:, half, g, :], qs[j][:, half, g, :], mark))
+                flush(1)
+
+        def q_step(j, g, halves):
+            old = len(late)
+            for half in halves:
+                q_unit(j, g, half)
+            while done["late"] < old:
+                run(late[done["late"]])
+                done["late"] += 1
+            nxt = 4 * j + g + 3
+            if nxt < 8:
+                widen(nxt // 4, nxt % 4)
+
+        def v_unit(g):
+            late.append((il_v(g), vc[:, g, :], vs[:, g, :], None))
 
         widen(0, 0)
         widen(0, 1)
+        widen(0, 2)
 
-        prev = None
         for g in range(G):
-            il = il_k(g)
-            if prev is not None:
-                quantize(prev[0], kc[:, prev[1], :], ks[:, prev[1], :])
-            prev = (il, g)
-        quantize(prev[0], kc[:, prev[1], :], ks[:, prev[1], :])
+            pending.append((il_k(g), kc[:, g, :], ks[:, g, :], None))
+            flush(1)
 
+        q_step(0, 0, (0, 1))
+        q_step(0, 1, (0, 1))
+
+        xgs = {}
         for tt in range(TT):
             words = x_sb[tt][:].bitcast(F32)
             xg = ilp.tile([P, 2048], BF16, name="xg", tag="il", align_bytes=64)
+            xgs[tt] = xg
             for gp in range(2):
                 xt = psum.tile([P, 512], F32, name="xt", tag="bank")
                 for gl in range(2):
@@ -253,50 +329,97 @@ def tile_diffucoderattention_pa_kernel(tc, hidden_states, Wq_bytes, Wq_scale, Wk
                             ident[:],
                         )
                 copy_on(
-                    "v" if gp == 0 else "s",
+                    "s" if (gp == 1 and tt % 2 == 0) else "v",
                     xg[:].bitcast(F32).rearrange("p (g r u) -> p g r u", g=G, u=2)[:, 2 * gp : 2 * gp + 2, :, :],
                     xt[:].rearrange("p (g u r) -> p g r u", g=2, u=2),
                 )
-            nc.vector.quantize_mx(out=xc[tt][:].bitcast(FP8X4), scales=xs[tt][:], in_=xg[:])
+            if tt == 0:
+                flush(0)
+            else:
+                nc.vector.quantize_mx(out=xc[tt - 1][:].bitcast(FP8X4), scales=xs[tt - 1][:], in_=xgs[tt - 1][:])
+        nc.vector.quantize_mx(out=xc[TT - 1][:].bitcast(FP8X4), scales=xs[TT - 1][:], in_=xgs[TT - 1][:])
+
+        def k_rot(tt):
+            return matmuls(tt, lambda g: kc[:, g, 0:256], lambda g: ks[:, g, 0:256], 256)
+
+        def k_plain(tt):
+            return matmuls(tt, lambda g: kc[:, g, 256:512], lambda g: ks[:, g, 256:512], 256)
+
+        def q_rot(j, tt):
+            return matmuls(tt, lambda g: qc[j][:, 0, g, :], lambda g: qs[j][:, 0, g, :], 512)
+
+        def q_plain(j, tt):
+            return matmuls(tt, lambda g: qc[j][:, 1, g, :], lambda g: qs[j][:, 1, g, :], 512)
+
+        k_r = {}
+        k_p = {}
+        for tt in range(TT):
+            k_r[tt] = k_rot(tt)
+        for tt in range(2):
+            k_p[tt] = k_plain(tt)
+
+        q_step(0, 2, (0, 1))
+        q_step(0, 3, (0, 1))
+        flush(0)
+
+        y_k = {}
+        for tt in range(TT):
+            y_k[tt] = xy.tile([P, 512], F32, name="y_k", tag="xy")
+            rope(tt, k_r[tt], 4, y_k[tt], nc.gpsimd)
+        for tt in range(TT):
+            if tt >= 2:
+                k_p[tt] = k_plain(tt)
+            plain(k_p[tt], 4, y_k[tt], "v")
+            nc.sync.dma_start(out=k_out[tt * P : (tt + 1) * P, :], in_=y_k[tt][:])
+        flush_late()
+
+        q_r = {}
+        q_p = {}
+        for tt in range(TT):
+            q_r[tt] = q_rot(0, tt)
+        for tt in range(2):
+            q_p[tt] = q_plain(0, tt)
+        v_unit(0)
+        v_unit(1)
+
+        q_step(1, 0, (0, 1))
+        flush(0)
+        flush_late()
+
+        y_q = {}
+        for tt in range(TT):
+            y_q[tt] = xy.tile([P, 1024], F32, name="y_q", tag="xy")
+            rope(tt, q_r[tt], 8, y_q[tt], nc.gpsimd)
+        for tt in range(TT):
+            if tt >= 2:
+                q_p[tt] = q_plain(0, tt)
+            plain(q_p[tt], 8, y_q[tt], "v" if tt < 2 else "s")
+            nc.sync.dma_start(out=q_out[tt * P : (tt + 1) * P, 0:1024], in_=y_q[tt][:])
 
         for tt in range(TT):
-            y = xy.tile([P, 512], F32, name="y_k", tag="xy")
-            acc = matmuls(tt, lambda g: kc[:, g, 0:256], lambda g: ks[:, g, 0:256], 256)
-            rope(tt, acc, 4, y)
-            acc = matmuls(tt, lambda g: kc[:, g, 256:512], lambda g: ks[:, g, 256:512], 256)
-            plain(acc, 4, y)
-            nc.sync.dma_start(out=k_out[tt * P : (tt + 1) * P, :], in_=y[:])
+            rot1["acc"][tt] = psum.tile([P, 512], F32, name="acc1", tag="bank")
+        rot1["open"] = True
+        rot1_passes()
+        v_unit(2)
+        v_unit(3)
 
-        for j in range(2):
-            prev = []
-            for g in range(G):
-                nxt = 4 * j + g + 2
-                if nxt < 8:
-                    widen(nxt // 4, nxt % 4)
-                cur = []
-                for half in range(2):
-                    cur.append((il_q(j, g, half), half, g))
-                for il, half, gg in prev:
-                    quantize(il, qc[j][:, half, gg, :], qs[j][:, half, gg, :])
-                prev = cur
-            for il, half, gg in prev:
-                quantize(il, qc[j][:, half, gg, :], qs[j][:, half, gg, :])
-
-            if j == 1:
-                for g in range(G):
-                    il = il_v(g)
-                    quantize(il, vc[:, g, :], vs[:, g, :])
-
-            for tt in range(TT):
-                y = xy.tile([P, 1024], F32, name="y_q", tag="xy")
-                acc = matmuls(tt, lambda g: qc[j][:, 0, g, :], lambda g: qs[j][:, 0, g, :], 512)
-                rope(tt, acc, 8, y)
-                acc = matmuls(tt, lambda g: qc[j][:, 1, g, :], lambda g: qs[j][:, 1, g, :], 512)
-                plain(acc, 8, y)
-                nc.sync.dma_start(out=q_out[tt * P : (tt + 1) * P, j * 1024 : (j + 1) * 1024], in_=y[:])
+        q_step(1, 1, (0, 1))
+        flush_late()
 
         for tt in range(TT):
             y = xy.tile([P, 512], F32, name="y_v", tag="xy")
             acc = matmuls(tt, lambda g: vc[:, g, :], lambda g: vs[:, g, :], 512)
-            copy_on("s" if tt % 2 == 0 else "v", y[:], acc[:])
+            copy_on("s", y[:], acc[:])
             nc.sync.dma_start(out=v_out[tt * P : (tt + 1) * P, :], in_=y[:])
+
+        q_step(1, 2, (0, 1))
+        q_step(1, 3, (1, 0))
+        flush(0)
+        flush_late()
+
+        for tt in range(TT):
+            y_q[tt] = xy.tile([P, 1024], F32, name="y_q", tag="xy")
+            rope(tt, rot1["acc"][tt], 8, y_q[tt], nc.gpsimd if tt < TT - 1 else nc.vector)
+            acc = q_plain(1, tt)
+            plain(acc, 8, y_q[tt], "s")
+            nc.sync.dma_start(out=q_out[tt * P : (tt + 1) * P, 1024:2048], in_=y_q[tt][:])

@@ -25,7 +25,8 @@ FREQ_STEP = 10000.0 ** (-1.0 / 32.0)
 TWO_PI_HI = 6.28125
 TWO_PI_LO = 2.0 * math.pi - TWO_PI_HI
 
-TENSOR_Q_UNITS = ((0, 1), (0, 3), (1, 0), (1, 1), (1, 2))
+SCALAR_Q_HALVES = ((1, 3, 1),)
+VECTOR_X_COPIES = ((0, 0), (1, 0), (2, 0), (3, 0))
 
 
 def tile_diffucoderattention_pa_kernel(tc, hidden_states, Wq_bytes, Wq_scale, Wk, Wv, out_0, out_1, out_2):
@@ -43,10 +44,10 @@ def tile_diffucoderattention_pa_kernel(tc, hidden_states, Wq_bytes, Wq_scale, Wk
         raw = ctx.enter_context(tc.tile_pool(name="raw", bufs=1))
         keep = ctx.enter_context(tc.tile_pool(name="keep", bufs=1))
         xy = ctx.enter_context(tc.tile_pool(name="xy", bufs=6))
-        widep = ctx.enter_context(tc.tile_pool(name="widep", bufs=3))
-        ilp = ctx.enter_context(tc.tile_pool(name="ilp", bufs=4))
+        widep = ctx.enter_context(tc.tile_pool(name="widep", bufs=4))
+        ilp = ctx.enter_context(tc.tile_pool(name="ilp", bufs=3))
         zp = ctx.enter_context(tc.tile_pool(name="zp", bufs=3))
-        psum = ctx.enter_context(tc.psum_pool(name="psum", bufs=6))
+        psum = ctx.enter_context(tc.psum_pool(name="psum", bufs=4))
 
         scl = const.tile([P, G * PACK], F32, name="scl")
         nc.sync.dma_start(
@@ -58,18 +59,18 @@ def tile_diffucoderattention_pa_kernel(tc, hidden_states, Wq_bytes, Wq_scale, Wk
         wv_raw = {}
         x_sb = {}
 
-        def load_q(j, g):
-            tl = raw.tile([P, PACK, 1024], U8, name="wq_bytes_%d_%d" % (j, g))
-            nc.sync.dma_start(out=tl[:], in_=wq_view[g][:, :, j * 1024 : (j + 1) * 1024])
-            wq_bytes[(j, g)] = tl
+        def load_q(j, g, th):
+            tl = raw.tile([P, 2, 1024], U8, name="wq_bytes_%d_%d_%d" % (j, g, th))
+            nc.sync.dma_start(out=tl[:], in_=wq_view[g][:, 2 * th : 2 * th + 2, j * 1024 : (j + 1) * 1024])
+            wq_bytes[(j, g, th)] = tl
 
         def load_k(g):
-            tl = raw.tile([P, PACK, 512], BF16, name="wk_raw_%d" % g)
+            tl = raw.tile([P, PACK, 512], BF16, name="wk_raw", tag="wkv", bufs=4)
             nc.sync.dma_start(out=tl[:], in_=wk_view[g])
             wk_raw[g] = tl
 
         def load_v(g):
-            tl = raw.tile([P, PACK, 512], BF16, name="wv_raw_%d" % g)
+            tl = raw.tile([P, PACK, 512], BF16, name="wv_raw", tag="wkv", bufs=4)
             nc.sync.dma_start(out=tl[:], in_=wv_view[g])
             wv_raw[g] = tl
 
@@ -78,24 +79,23 @@ def tile_diffucoderattention_pa_kernel(tc, hidden_states, Wq_bytes, Wq_scale, Wk
             nc.sync.dma_start(out=tl[:], in_=x_rows[tt * P : (tt + 1) * P, :])
             x_sb[tt] = tl
 
-        load_q(0, 0)
+        load_q(0, 0, 0)
         load_k(0)
+        load_q(0, 0, 1)
         load_k(1)
-        load_q(0, 1)
         load_k(2)
+        load_q(0, 1, 0)
+        load_q(0, 1, 1)
         load_k(3)
-        load_q(0, 2)
         load_x(0)
         load_x(1)
-        load_q(0, 3)
+        load_q(0, 2, 0)
+        load_q(0, 2, 1)
         load_x(2)
         load_x(3)
-        load_q(1, 0)
-        load_q(1, 1)
-        for g in range(G):
-            load_v(g)
-        load_q(1, 2)
-        load_q(1, 3)
+        for j, g in ((0, 3), (1, 0), (1, 1)):
+            load_q(j, g, 0)
+            load_q(j, g, 1)
 
         warm = const.tile([P, 2], F32, name="warm")
         nc.vector.memset(warm[:], 0.0)
@@ -103,8 +103,6 @@ def tile_diffucoderattention_pa_kernel(tc, hidden_states, Wq_bytes, Wq_scale, Wk
 
         ident = const.tile([P, P], F32, name="ident")
         make_identity(nc, ident[:])
-        ident_bf = const.tile([P, P], BF16, name="ident_bf")
-        make_identity(nc, ident_bf[:])
 
         pos = const.tile([P, TT], F32, name="pos")
         nc.gpsimd.iota(pos[:], pattern=[[P, TT]], base=0, channel_multiplier=1, allow_small_or_imprecise_dtypes=True)
@@ -139,27 +137,22 @@ def tile_diffucoderattention_pa_kernel(tc, hidden_states, Wq_bytes, Wq_scale, Wk
 
         xc = {}
         xs = {}
-        for tt in range(TT):
-            xc[tt] = keep.tile([P, G * P], U32, name="xc_%d" % tt, align_bytes=64)
-            xs[tt] = keep.tile([P, G * P], U8, name="xs_%d" % tt, align_bytes=64)
+        for tp in range(2):
+            xc[tp] = keep.tile([P, 2 * G * P], U32, name="xc_%d" % tp, align_bytes=64)
+            xs[tp] = keep.tile([P, 2 * G * P], U8, name="xs_%d" % tp, align_bytes=64)
         qc = {}
         qs = {}
         for j in range(2):
-            qc[j] = keep.tile([P, 2, G, 512], U32, name="qc_%d" % j, align_bytes=64)
-            qs[j] = keep.tile([P, 2, G, 512], U8, name="qs_%d" % j, align_bytes=64)
-        kc = keep.tile([P, G, 512], U32, name="kc", align_bytes=64)
-        ks = keep.tile([P, G, 512], U8, name="ks", align_bytes=64)
-        vc = keep.tile([P, G, 512], U32, name="vc", align_bytes=64)
-        vs = keep.tile([P, G, 512], U8, name="vs", align_bytes=64)
+            qc[j] = keep.tile([P, G, 1024], U32, name="qc_%d" % j, align_bytes=64)
+            qs[j] = keep.tile([P, G, 1024], U8, name="qs_%d" % j, align_bytes=64)
+        kc = keep.tile([P, G, 512], U32, name="kc", tag="kvc", align_bytes=64)
+        ks = keep.tile([P, G, 512], U8, name="ks", tag="kvs", align_bytes=64)
 
         def copy_on(eng, out, in_):
             if eng == "v":
                 nc.vector.tensor_copy(out=out, in_=in_)
             else:
                 nc.scalar.copy(out=out, in_=in_)
-
-        def quantize(il, codes, scales):
-            nc.vector.quantize_mx(out=codes.bitcast(FP8X4), scales=scales, in_=il[:])
 
         wide = {}
 
@@ -168,258 +161,243 @@ def tile_diffucoderattention_pa_kernel(tc, hidden_states, Wq_bytes, Wq_scale, Wk
             for t in range(PACK):
                 nc.scalar.activation(
                     out=tl[:, t, :],
-                    in_=wq_bytes[(j, g)][:, t, :].bitcast(FP8),
+                    in_=wq_bytes[(j, g, t // 2)][:, t % 2, :].bitcast(FP8),
                     func=ACT.Copy,
                     scale=scl[:, PACK * g + t : PACK * g + t + 1],
                 )
             wide[(j, g)] = tl
 
-        def il_q(j, g, half):
-            il = ilp.tile([P, 2048], BF16, name="il", tag="il", align_bytes=64)
-            src = wide[(j, g)][:].rearrange("p t (h c i) -> p h c t i", h=8, i=4)[:, :, half * 16 : (half + 1) * 16, :, :]
-            dst = il[:].rearrange("p (h c i t) -> p h c t i", h=8, i=4, t=PACK)
-            copy_on("v", dst, src)
-            return il
+        def il_heads(eng, dst, planes, heads, half):
+            copy_on(
+                eng,
+                dst.rearrange("p (h c i t) -> p h c t i", h=heads, i=4, t=PACK),
+                planes.rearrange("p t (h c i) -> p h c t i", h=heads, i=4)[:, :, half * 16 : (half + 1) * 16, :, :],
+            )
 
-        def il_tensor(view):
-            il = ilp.tile([P, 2048], BF16, name="ilt", tag="ilt", bufs=3, align_bytes=64)
-            for b in range(2):
-                st = psum.tile([P, 1024], BF16, name="st", tag="stage", bufs=2)
-                for m in range(2):
-                    nc.tensor.matmul(out=st[:, m * 512 : (m + 1) * 512], lhsT=ident_bf[:], rhs=view(2 * b + m), start=True, stop=True)
-                nc.scalar.copy(out=il[:, b * 1024 : (b + 1) * 1024], in_=st[:])
-            return il
-
-        def il_q_tensor(j, g):
-            planes = wide[(j, g)][:].rearrange("p t (h f) -> p h f t", f=128)
-            return il_tensor(lambda m: planes[:, 2 * m : 2 * m + 2, 64:128, :])
-
-        def il_k(g):
-            il = ilp.tile([P, 2048], BF16, name="il", tag="il", align_bytes=64)
+        def il_q(j, g):
+            il = ilp.tile([P, 4096], BF16, name="il", tag="il", align_bytes=64)
             for half in range(2):
-                src = wk_raw[g][:].rearrange("p t (h c i) -> p h c t i", h=4, i=4)[:, :, half * 16 : (half + 1) * 16, :, :]
-                dst = il[:, half * 1024 : (half + 1) * 1024].rearrange("p (h c i t) -> p h c t i", h=4, i=4, t=PACK)
-                copy_on("v", dst, src)
+                il_heads("s" if (j, g, half) in SCALAR_Q_HALVES else "v", il[:, half * 2048 : (half + 1) * 2048], wide[(j, g)][:], 8, half)
             return il
 
-        def il_v(g):
-            planes = wv_raw[g][:].rearrange("p t n -> p n t")
-            return il_tensor(lambda m: planes[:, m * P : (m + 1) * P, :])
-
-        def one_pass(acc, tt, g, codes, scales, n):
-            if True:
-                nc.tensor.matmul_mx(
-                    out=acc[:, 0:n],
-                    lhsT=xc[tt][:, g * P : (g + 1) * P].bitcast(FP8X4),
-                    lhsT_scale=xs[tt][:, g * P : (g + 1) * P],
-                    rhs=codes(g).bitcast(FP8X4),
-                    rhs_scale=scales(g),
-                    start=(g == 0),
-                    stop=(g == G - 1),
+        def il_k(gp):
+            il = ilp.tile([P, 4096], BF16, name="il", tag="il", align_bytes=64)
+            for gl in range(2):
+                copy_on(
+                    "v",
+                    il[:, gl * 2048 : (gl + 1) * 2048].rearrange("p (c i t) -> p c t i", i=4, t=PACK),
+                    wk_raw[2 * gp + gl][:].rearrange("p t (c i) -> p c t i", i=4),
                 )
+            return il
 
-        def matmuls(tt, codes, scales, n):
-            acc = psum.tile([P, 512], F32, name="acc", tag="bank")
+        def il_v(gp):
+            il = ilp.tile([P, 4096], BF16, name="ilt", tag="ilt", bufs=2, align_bytes=64)
+            for gl in range(2):
+                copy_on(
+                    "s",
+                    il[:, gl * 2048 : (gl + 1) * 2048].rearrange("p (c i t) -> p c t i", i=4, t=PACK),
+                    wv_raw[2 * gp + gl][:].rearrange("p t (c i) -> p c t i", i=4),
+                )
+            return il
+
+        def one_pass(acc, tt, g, codes, scales):
+            lo = (tt % 2) * 512 + g * P
+            nc.tensor.matmul_mx(
+                out=acc,
+                lhsT=xc[tt // 2][:, lo : lo + P].bitcast(FP8X4),
+                lhsT_scale=xs[tt // 2][:, lo : lo + P],
+                rhs=codes[:, g, :].bitcast(FP8X4),
+                rhs_scale=scales[:, g, :],
+                start=(g == 0),
+                stop=(g == G - 1),
+            )
+
+        def matmuls(tt, codes, scales, side):
+            n = codes.shape[2]
+            acc = psum.tile([P, 512], F32, name="acc", tag=side)
             for g in range(G):
-                one_pass(acc, tt, g, codes, scales, n)
+                one_pass(acc[:, 0:n], tt, g, codes, scales)
             return acc
 
-        def rope(tt, acc, heads, y, add_eng):
+        def heads_of(ap, width):
+            return ap.rearrange("p (h f) -> p h f", f=width)
+
+        def rope(tt, rot, y_rot, add_eng):
+            heads = rot.shape[1]
             n = heads * 64
             z = zp.tile([P, 2, 512], F32, name="z", tag="z")
             shape = [P, heads, PAIRS, 2]
             for r in range(2):
                 nc.vector.tensor_tensor(
                     out=z[:, r, 0:n].rearrange("p (h i e) -> p h i e", h=heads, e=2),
-                    in0=acc[:, 0:n].rearrange("p (h i e) -> p h i e", h=heads, e=2)[:, :, :, r : r + 1].to_broadcast(shape),
+                    in0=rot.rearrange("p h (i e) -> p h i e", e=2)[:, :, :, r : r + 1].to_broadcast(shape),
                     in1=tab[:, tt, r, :, :].unsqueeze(1).to_broadcast(shape),
                     op=ALU.mult,
                 )
-            add_eng.tensor_tensor(
-                out=y[:].rearrange("p (h f) -> p h f", f=128)[:, :, 0:64],
-                in0=z[:, 0, 0:n].rearrange("p (h f) -> p h f", f=64),
-                in1=z[:, 1, 0:n].rearrange("p (h f) -> p h f", f=64),
-                op=ALU.add,
-            )
+            add_eng.tensor_tensor(out=y_rot, in0=heads_of(z[:, 0, 0:n], 64), in1=heads_of(z[:, 1, 0:n], 64), op=ALU.add)
 
-        def plain(acc, heads, y, eng):
-            copy_on(
-                eng,
-                y[:].rearrange("p (h f) -> p h f", f=128)[:, :, 64:128],
-                acc[:, 0 : heads * 64].rearrange("p (h f) -> p h f", f=64),
-            )
-
-        ctx.enter_context(tc.manual_schedule(engines={mybir.EngineType.DVE, mybir.EngineType.Pool}))
+        ctx.enter_context(tc.manual_schedule())
 
         pending = []
-        late = []
-        done = {"pending": 0, "late": 0}
-        rot1 = {"open": False, "ready": [], "acc": {}}
+        done = {"pending": 0}
+        step_groups = []
+        ready = []
 
-        def rot1_passes():
-            if rot1["open"]:
-                for g in rot1["ready"]:
-                    for tt in range(TT):
-                        one_pass(rot1["acc"][tt], tt, g, lambda gg: qc[1][:, 0, gg, :], lambda gg: qs[1][:, 0, gg, :], 512)
-                rot1["ready"].clear()
+        def open_group(lo, side):
+            accs = []
+            for tt in range(TT):
+                acc1 = psum.tile([P, 512], F32, name="acc1", tag=side)
+                accs.append(acc1)
+            for tt in range(TT):
+                for g in ready:
+                    one_pass(accs[tt][:], tt, g, qc[1][:, :, lo : lo + 512], qs[1][:, :, lo : lo + 512])
+            step_groups.append((lo, accs))
+            return accs
 
         def run(unit):
-            il, codes, scales, mark = unit
-            quantize(il, codes, scales)
-            if mark is not None:
-                rot1["ready"].append(mark)
-                rot1_passes()
+            il, codes, scales, g = unit
+            nc.vector.quantize_mx(out=codes.bitcast(FP8X4), scales=scales, in_=il[:])
+            if g is not None:
+                ready.append(g)
+                for lo, accs in step_groups:
+                    for tt in range(TT):
+                        one_pass(accs[tt][:], tt, g, qc[1][:, :, lo : lo + 512], qs[1][:, :, lo : lo + 512])
 
-        def flush(keep):
-            while len(pending) - done["pending"] > keep:
+        def flush(keep_back):
+            while len(pending) - done["pending"] > keep_back:
                 run(pending[done["pending"]])
                 done["pending"] += 1
 
-        def flush_late():
-            while len(late) - done["late"] > 0:
-                run(late[done["late"]])
-                done["late"] += 1
+        def q_step(j, g):
+            pending.append((il_q(j, g), qc[j][:, g, :], qs[j][:, g, :], g if j == 1 else None))
+            flush(1)
 
-        def q_unit(j, g, half):
-            mark = g if (j == 1 and half == 0) else None
-            if half == 1 and (j, g) in TENSOR_Q_UNITS:
-                late.append((il_q_tensor(j, g), qc[j][:, half, g, :], qs[j][:, half, g, :], mark))
-            else:
-                pending.append((il_q(j, g, half), qc[j][:, half, g, :], qs[j][:, half, g, :], mark))
-                flush(1)
+        def turn_x(tp):
+            xg = ilp.tile([P, 4096], BF16, name="xg", tag="il", align_bytes=64)
+            xg_words = xg[:].bitcast(F32).rearrange("p (a g r u) -> p a g r u", a=2, g=G, u=2)
+            for a in range(2):
+                tt = 2 * tp + a
+                words = x_sb[tt][:].bitcast(F32)
+                for gp in range(2):
+                    xt = psum.tile([P, 512], F32, name="xt", tag="A" if gp == 0 else "B")
+                    for gl in range(2):
+                        g = 2 * gp + gl
+                        for u in range(2):
+                            nc.tensor.transpose(
+                                xt[:, (2 * gl + u) * P : (2 * gl + u + 1) * P],
+                                words[:, 256 * g + u : 256 * (g + 1) : 2],
+                                ident[:],
+                            )
+                    copy_on(
+                        "v" if gp == 0 else "s",
+                        xg_words[:, a, 2 * gp : 2 * gp + 2, :, :],
+                        xt[:].rearrange("p (g u r) -> p g r u", g=2, u=2),
+                    )
+            pending.append((xg, xc[tp][:], xs[tp][:], None))
+            flush(1)
 
-        def q_step(j, g, halves):
-            old = len(late)
-            for half in halves:
-                q_unit(j, g, half)
-            while done["late"] < old:
-                run(late[done["late"]])
-                done["late"] += 1
-            nxt = 4 * j + g + 3
-            if nxt < 8:
-                widen(nxt // 4, nxt % 4)
-
-        def v_unit(g):
-            late.append((il_v(g), vc[:, g, :], vs[:, g, :], None))
+        def k_unit(gp):
+            pending.append((
+                il_k(gp),
+                kc[:, 2 * gp : 2 * gp + 2, :].rearrange("p g n -> p (g n)"),
+                ks[:, 2 * gp : 2 * gp + 2, :].rearrange("p g n -> p (g n)"),
+                None,
+            ))
+            flush(1)
 
         widen(0, 0)
         widen(0, 1)
-        widen(0, 2)
-
+        k_unit(0)
+        k_unit(1)
         for g in range(G):
-            pending.append((il_k(g), kc[:, g, :], ks[:, g, :], None))
-            flush(1)
+            load_v(g)
+        for g in (2, 3):
+            load_q(1, g, 0)
+            load_q(1, g, 1)
+        q_step(0, 0)
+        turn_x(0)
+        widen(0, 2)
+        q_step(0, 1)
+        turn_x(1)
+        widen(0, 3)
+        q_step(0, 2)
+        widen(1, 0)
 
-        q_step(0, 0, (0, 1))
-        q_step(0, 1, (0, 1))
-
-        xgs = {}
+        k_acc = {}
         for tt in range(TT):
-            words = x_sb[tt][:].bitcast(F32)
-            xg = ilp.tile([P, 2048], BF16, name="xg", tag="il", align_bytes=64)
-            xgs[tt] = xg
-            for gp in range(2):
-                xt = psum.tile([P, 512], F32, name="xt", tag="bank")
-                for gl in range(2):
-                    g = 2 * gp + gl
-                    for u in range(2):
-                        nc.tensor.transpose(
-                            xt[:, (2 * gl + u) * P : (2 * gl + u + 1) * P],
-                            words[:, 256 * g + u : 256 * (g + 1) : 2],
-                            ident[:],
-                        )
-                copy_on(
-                    "s" if (gp == 1 and tt % 2 == 0) else "v",
-                    xg[:].bitcast(F32).rearrange("p (g r u) -> p g r u", g=G, u=2)[:, 2 * gp : 2 * gp + 2, :, :],
-                    xt[:].rearrange("p (g u r) -> p g r u", g=2, u=2),
-                )
-            if tt == 0:
-                flush(0)
-            else:
-                nc.vector.quantize_mx(out=xc[tt - 1][:].bitcast(FP8X4), scales=xs[tt - 1][:], in_=xgs[tt - 1][:])
-        nc.vector.quantize_mx(out=xc[TT - 1][:].bitcast(FP8X4), scales=xs[TT - 1][:], in_=xgs[TT - 1][:])
+            k_acc[tt] = matmuls(tt, kc[:, :, :], ks[:, :, :], "A")
 
-        def k_rot(tt):
-            return matmuls(tt, lambda g: kc[:, g, 0:256], lambda g: ks[:, g, 0:256], 256)
-
-        def k_plain(tt):
-            return matmuls(tt, lambda g: kc[:, g, 256:512], lambda g: ks[:, g, 256:512], 256)
-
-        def q_rot(j, tt):
-            return matmuls(tt, lambda g: qc[j][:, 0, g, :], lambda g: qs[j][:, 0, g, :], 512)
-
-        def q_plain(j, tt):
-            return matmuls(tt, lambda g: qc[j][:, 1, g, :], lambda g: qs[j][:, 1, g, :], 512)
-
-        k_r = {}
-        k_p = {}
-        for tt in range(TT):
-            k_r[tt] = k_rot(tt)
-        for tt in range(2):
-            k_p[tt] = k_plain(tt)
-
-        q_step(0, 2, (0, 1))
-        q_step(0, 3, (0, 1))
-        flush(0)
+        il_v0 = il_v(0)
+        q_step(0, 3)
+        widen(1, 1)
 
         y_k = {}
         for tt in range(TT):
             y_k[tt] = xy.tile([P, 512], F32, name="y_k", tag="xy")
-            rope(tt, k_r[tt], 4, y_k[tt], nc.gpsimd)
+            rope(tt, heads_of(k_acc[tt][:], 128)[:, :, 0:64], heads_of(y_k[tt][:], 128)[:, :, 0:64], nc.gpsimd)
         for tt in range(TT):
-            if tt >= 2:
-                k_p[tt] = k_plain(tt)
-            plain(k_p[tt], 4, y_k[tt], "v")
+            copy_on("v" if tt < 2 else "s", heads_of(y_k[tt][:], 128)[:, :, 64:128], heads_of(k_acc[tt][:], 128)[:, :, 64:128])
             nc.sync.dma_start(out=k_out[tt * P : (tt + 1) * P, :], in_=y_k[tt][:])
-        flush_late()
+
+        q_step(1, 0)
+        widen(1, 2)
 
         q_r = {}
         q_p = {}
         for tt in range(TT):
-            q_r[tt] = q_rot(0, tt)
-        for tt in range(2):
-            q_p[tt] = q_plain(0, tt)
-        v_unit(0)
-        v_unit(1)
+            q_r[tt] = matmuls(tt, qc[0][:, :, 0:512], qs[0][:, :, 0:512], "A")
+        for tt in range(TT):
+            q_p[tt] = matmuls(tt, qc[0][:, :, 512:1024], qs[0][:, :, 512:1024], "B")
 
-        q_step(1, 0, (0, 1))
+        vc = keep.tile([P, G, 512], U32, name="vc", tag="kvc", align_bytes=64)
+        vs = keep.tile([P, G, 512], U8, name="vs", tag="kvs", align_bytes=64)
+
+        def quantize_v(gp, il):
+            nc.vector.quantize_mx(
+                out=vc[:, 2 * gp : 2 * gp + 2, :].rearrange("p g n -> p (g n)").bitcast(FP8X4),
+                scales=vs[:, 2 * gp : 2 * gp + 2, :].rearrange("p g n -> p (g n)"),
+                in_=il[:],
+            )
+
+        quantize_v(0, il_v0)
         flush(0)
-        flush_late()
+        il_v1 = il_v(1)
+        widen(1, 3)
 
         y_q = {}
         for tt in range(TT):
             y_q[tt] = xy.tile([P, 1024], F32, name="y_q", tag="xy")
-            rope(tt, q_r[tt], 8, y_q[tt], nc.gpsimd)
+            rope(tt, heads_of(q_r[tt][:], 64), heads_of(y_q[tt][:], 128)[:, :, 0:64], nc.gpsimd)
         for tt in range(TT):
-            if tt >= 2:
-                q_p[tt] = q_plain(0, tt)
-            plain(q_p[tt], 8, y_q[tt], "v" if tt < 2 else "s")
+            copy_on("v", heads_of(y_q[tt][:], 128)[:, :, 64:128], heads_of(q_p[tt][:], 64))
             nc.sync.dma_start(out=q_out[tt * P : (tt + 1) * P, 0:1024], in_=y_q[tt][:])
 
+        rot_acc = open_group(0, "A")
+
+        q_step(1, 1)
+        quantize_v(1, il_v1)
+        v_acc = {}
         for tt in range(TT):
-            rot1["acc"][tt] = psum.tile([P, 512], F32, name="acc1", tag="bank")
-        rot1["open"] = True
-        rot1_passes()
-        v_unit(2)
-        v_unit(3)
-
-        q_step(1, 1, (0, 1))
-        flush_late()
-
-        for tt in range(TT):
-            y = xy.tile([P, 512], F32, name="y_v", tag="xy")
-            acc = matmuls(tt, lambda g: vc[:, g, :], lambda g: vs[:, g, :], 512)
-            copy_on("s", y[:], acc[:])
-            nc.sync.dma_start(out=v_out[tt * P : (tt + 1) * P, :], in_=y[:])
-
-        q_step(1, 2, (0, 1))
-        q_step(1, 3, (1, 0))
+            v_acc[tt] = matmuls(tt, vc[:, :, :], vs[:, :, :], "B")
+        q_step(1, 2)
+        q_step(1, 3)
         flush(0)
-        flush_late()
+        for tt in range(TT):
+            y = xy.tile([P, 512], F32, name="y_v", tag="y_v", bufs=4)
+            copy_on("s", y[:], v_acc[tt][:])
+            nc.sync.dma_start(out=v_out[tt * P : (tt + 1) * P, :], in_=y[:])
+        plain_acc = open_group(512, "B")
 
         for tt in range(TT):
             y_q[tt] = xy.tile([P, 1024], F32, name="y_q", tag="xy")
-            rope(tt, rot1["acc"][tt], 8, y_q[tt], nc.gpsimd if tt < TT - 1 else nc.vector)
-            acc = q_plain(1, tt)
-            plain(acc, 8, y_q[tt], "s")
-            nc.sync.dma_start(out=q_out[tt * P : (tt + 1) * P, 1024:2048], in_=y_q[tt][:])
+            copy_on("s", heads_of(y_q[tt][:], 128)[:, :, 64:128], heads_of(plain_acc[tt][:], 64))
+            rot = heads_of(rot_acc[tt][:], 64)
+            y_rot = heads_of(y_q[tt][:], 128)[:, :, 0:64]
+            if tt < TT - 1:
+                rope(tt, rot, y_rot, nc.gpsimd)
+                nc.sync.dma_start(out=q_out[tt * P : (tt + 1) * P, 1024:2048], in_=y_q[tt][:])
+            else:
+                rope(tt, rot[:, 0:4, :], y_rot[:, 0:4, :], nc.vector)
+                nc.sync.dma_start(out=q_out[tt * P : (tt + 1) * P, 1024:1536], in_=y_q[tt][:, 0:512])
+                rope(tt, rot[:, 4:8, :], y_rot[:, 4:8, :], nc.vector)
+                nc.sync.dma_start(out=q_out[tt * P : (tt + 1) * P, 1536:2048], in_=y_q[tt][:, 512:1024])

@@ -83,17 +83,19 @@ def tile_diffucoderattention_pa_kernel(tc, hidden_states, Wq_bytes, Wq_scale, Wk
         load_k(0)
         load_q(0, 0, 1)
         load_k(1)
-        load_k(2)
         load_q(0, 1, 0)
         load_q(0, 1, 1)
+        load_k(2)
         load_k(3)
-        load_x(0)
-        load_x(1)
         load_q(0, 2, 0)
         load_q(0, 2, 1)
+        load_x(0)
+        load_x(1)
+        load_q(0, 3, 0)
+        load_q(0, 3, 1)
         load_x(2)
         load_x(3)
-        for j, g in ((0, 3), (1, 0), (1, 1)):
+        for j, g in ((1, 0), (1, 1)):
             load_q(j, g, 0)
             load_q(j, g, 1)
 
@@ -222,7 +224,7 @@ def tile_diffucoderattention_pa_kernel(tc, hidden_states, Wq_bytes, Wq_scale, Wk
         def heads_of(ap, width):
             return ap.rearrange("p (h f) -> p h f", f=width)
 
-        def rope(tt, rot, y_rot, add_eng):
+        def rope_products(tt, rot):
             heads = rot.shape[1]
             n = heads * 64
             z = zp.tile([P, 2, 512], F32, name="z", tag="z")
@@ -234,7 +236,13 @@ def tile_diffucoderattention_pa_kernel(tc, hidden_states, Wq_bytes, Wq_scale, Wk
                     in1=tab[:, tt, r, :, :].unsqueeze(1).to_broadcast(shape),
                     op=ALU.mult,
                 )
-            add_eng.tensor_tensor(out=y_rot, in0=heads_of(z[:, 0, 0:n], 64), in1=heads_of(z[:, 1, 0:n], 64), op=ALU.add)
+            return z[:, :, 0:n]
+
+        def rope_sum(z, y_rot, add_eng):
+            add_eng.tensor_tensor(out=y_rot, in0=heads_of(z[:, 0, :], 64), in1=heads_of(z[:, 1, :], 64), op=ALU.add)
+
+        def rope(tt, rot, y_rot, add_eng):
+            rope_sum(rope_products(tt, rot), y_rot, add_eng)
 
         ctx.enter_context(tc.manual_schedule())
 
@@ -308,19 +316,21 @@ def tile_diffucoderattention_pa_kernel(tc, hidden_states, Wq_bytes, Wq_scale, Wk
         widen(0, 0)
         widen(0, 1)
         k_unit(0)
+        flush(0)
+        q_step(0, 0)
         k_unit(1)
         for g in range(G):
             load_v(g)
         for g in (2, 3):
             load_q(1, g, 0)
             load_q(1, g, 1)
-        q_step(0, 0)
-        turn_x(0)
         widen(0, 2)
         q_step(0, 1)
-        turn_x(1)
+        turn_x(0)
         widen(0, 3)
         q_step(0, 2)
+        turn_x(1)
+        flush(0)
         widen(1, 0)
 
         k_acc = {}
@@ -364,6 +374,8 @@ def tile_diffucoderattention_pa_kernel(tc, hidden_states, Wq_bytes, Wq_scale, Wk
         il_v1 = il_v(1)
         widen(1, 3)
 
+        q_step(1, 1)
+
         y_q = {}
         for tt in range(TT):
             y_q[tt] = xy.tile([P, 1024], F32, name="y_q", tag="xy")
@@ -374,7 +386,6 @@ def tile_diffucoderattention_pa_kernel(tc, hidden_states, Wq_bytes, Wq_scale, Wk
 
         rot_acc = open_group(0, "A")
 
-        q_step(1, 1)
         quantize_v(1, il_v1)
         v_acc = {}
         for tt in range(TT):
@@ -397,7 +408,9 @@ def tile_diffucoderattention_pa_kernel(tc, hidden_states, Wq_bytes, Wq_scale, Wk
                 rope(tt, rot, y_rot, nc.gpsimd)
                 nc.sync.dma_start(out=q_out[tt * P : (tt + 1) * P, 1024:2048], in_=y_q[tt][:])
             else:
-                rope(tt, rot[:, 0:4, :], y_rot[:, 0:4, :], nc.vector)
+                z_lo = rope_products(tt, rot[:, 0:4, :])
+                z_hi = rope_products(tt, rot[:, 4:8, :])
+                rope_sum(z_lo, y_rot[:, 0:4, :], nc.vector)
                 nc.sync.dma_start(out=q_out[tt * P : (tt + 1) * P, 1024:1536], in_=y_q[tt][:, 0:512])
-                rope(tt, rot[:, 4:8, :], y_rot[:, 4:8, :], nc.vector)
+                rope_sum(z_hi, y_rot[:, 4:8, :], nc.vector)
                 nc.sync.dma_start(out=q_out[tt * P : (tt + 1) * P, 1536:2048], in_=y_q[tt][:, 512:1024])

@@ -26,6 +26,7 @@ TWO_PI_HI = 6.28125
 TWO_PI_LO = 2.0 * math.pi - TWO_PI_HI
 
 SCALAR_Q_HALVES = ((1, 3, 1),)
+RUN = 8
 VECTOR_X_COPIES = ((0, 0), (1, 0), (2, 0), (3, 0))
 
 
@@ -172,8 +173,8 @@ def tile_diffucoderattention_pa_kernel(tc, hidden_states, Wq_bytes, Wq_scale, Wk
         def il_heads(eng, dst, planes, heads, half):
             copy_on(
                 eng,
-                dst.rearrange("p (h c i t) -> p h c t i", h=heads, i=4, t=PACK),
-                planes.rearrange("p t (h c i) -> p h c t i", h=heads, i=4)[:, :, half * 16 : (half + 1) * 16, :, :],
+                dst.rearrange("p (h c i t) -> p h c t i", h=heads, i=RUN, t=PACK),
+                planes.rearrange("p t (h c i) -> p h c t i", h=heads, i=RUN)[:, :, half * (64 // RUN) : (half + 1) * (64 // RUN), :, :],
             )
 
         def il_q(j, g):
@@ -187,8 +188,8 @@ def tile_diffucoderattention_pa_kernel(tc, hidden_states, Wq_bytes, Wq_scale, Wk
             for gl in range(2):
                 copy_on(
                     "v",
-                    il[:, gl * 2048 : (gl + 1) * 2048].rearrange("p (c i t) -> p c t i", i=4, t=PACK),
-                    wk_raw[2 * gp + gl][:].rearrange("p t (c i) -> p c t i", i=4),
+                    il[:, gl * 2048 : (gl + 1) * 2048].rearrange("p (c i t) -> p c t i", i=RUN, t=PACK),
+                    wk_raw[2 * gp + gl][:].rearrange("p t (c i) -> p c t i", i=RUN),
                 )
             return il
 
@@ -197,8 +198,8 @@ def tile_diffucoderattention_pa_kernel(tc, hidden_states, Wq_bytes, Wq_scale, Wk
             for gl in range(2):
                 copy_on(
                     "s",
-                    il[:, gl * 2048 : (gl + 1) * 2048].rearrange("p (c i t) -> p c t i", i=4, t=PACK),
-                    wv_raw[2 * gp + gl][:].rearrange("p t (c i) -> p c t i", i=4),
+                    il[:, gl * 2048 : (gl + 1) * 2048].rearrange("p (c i t) -> p c t i", i=RUN, t=PACK),
+                    wv_raw[2 * gp + gl][:].rearrange("p t (c i) -> p c t i", i=RUN),
                 )
             return il
 

@@ -25,8 +25,10 @@ FREQ_STEP = 10000.0 ** (-1.0 / 32.0)
 TWO_PI_HI = 6.28125
 TWO_PI_LO = 2.0 * math.pi - TWO_PI_HI
 
-SCALAR_Q_HALVES = ((1, 3, 1),)
+SCALAR_Q_HALVES = ((1, 2, 1), (1, 3, 1))
 RUN = 8
+XENG = ("ss", "ss")
+VP = {(0, 3): (0, 1)}
 VECTOR_X_COPIES = ((0, 0), (1, 0), (2, 0), (3, 0))
 
 
@@ -106,6 +108,8 @@ def tile_diffucoderattention_pa_kernel(tc, hidden_states, Wq_bytes, Wq_scale, Wk
 
         ident = const.tile([P, P], F32, name="ident")
         make_identity(nc, ident[:])
+        ident_b = const.tile([P, P], BF16, name="ident_b")
+        make_identity(nc, ident_b[:])
 
         pos = const.tile([P, TT], F32, name="pos")
         nc.gpsimd.iota(pos[:], pattern=[[P, TT]], base=0, channel_multiplier=1, allow_small_or_imprecise_dtypes=True)
@@ -162,12 +166,12 @@ def tile_diffucoderattention_pa_kernel(tc, hidden_states, Wq_bytes, Wq_scale, Wk
         def widen(j, g):
             tl = widep.tile([P, PACK, 1024], BF16, name="wide", tag="wide")
             for t in range(PACK):
-                nc.scalar.activation(
-                    out=tl[:, t, :],
-                    in_=wq_bytes[(j, g, t // 2)][:, t % 2, :].bitcast(FP8),
-                    func=ACT.Copy,
-                    scale=scl[:, PACK * g + t : PACK * g + t + 1],
-                )
+                src = wq_bytes[(j, g, t // 2)][:, t % 2, :].bitcast(FP8)
+                col = scl[:, PACK * g + t : PACK * g + t + 1]
+                if t in VP.get((j, g), ()):
+                    nc.vector.tensor_scalar(out=tl[:, t, :], in0=src, scalar1=col, scalar2=None, op0=ALU.mult)
+                else:
+                    nc.scalar.activation(out=tl[:, t, :], in_=src, func=ACT.Copy, scale=col)
             wide[(j, g)] = tl
 
         def il_heads(eng, dst, planes, heads, half):
@@ -193,14 +197,26 @@ def tile_diffucoderattention_pa_kernel(tc, hidden_states, Wq_bytes, Wq_scale, Wk
                 )
             return il
 
-        def il_v(gp):
-            il = ilp.tile([P, 4096], BF16, name="ilt", tag="ilt", bufs=2, align_bytes=64)
+        def fill_v(gp):
+            banks = []
             for gl in range(2):
-                copy_on(
-                    "s",
-                    il[:, gl * 2048 : (gl + 1) * 2048].rearrange("p (c i t) -> p c t i", i=RUN, t=PACK),
-                    wv_raw[2 * gp + gl][:].rearrange("p t (c i) -> p c t i", i=RUN),
-                )
+                for b in range(2):
+                    bank = psum.tile([P, 1024], BF16, name="rt", tag="B")
+                    for k in range(2):
+                        nc.tensor.matmul(
+                            out=bank[:].rearrange("p (c t) -> p t c", t=PACK)[:, 2 * k : 2 * k + 2, :],
+                            lhsT=ident_b[:],
+                            rhs=wv_raw[2 * gp + gl][:, 2 * k : 2 * k + 2, b * 256 : (b + 1) * 256],
+                            start=True,
+                            stop=True,
+                        )
+                    banks.append(bank)
+            return banks
+
+        def empty_v(banks):
+            il = ilp.tile([P, 4096], BF16, name="ilt", tag="ilt", bufs=2, align_bytes=64)
+            for b in range(4):
+                copy_on("s", il[:, b * 1024 : (b + 1) * 1024].bitcast(F32), banks[b][:].bitcast(F32))
             return il
 
         def one_pass(acc, tt, g, codes, scales):
@@ -298,7 +314,7 @@ def tile_diffucoderattention_pa_kernel(tc, hidden_states, Wq_bytes, Wq_scale, Wk
                                 ident[:],
                             )
                     copy_on(
-                        "v" if gp == 0 else "s",
+                        XENG[tp][gp],
                         xg_words[:, a, 2 * gp : 2 * gp + 2, :, :],
                         xt[:].rearrange("p (g u r) -> p g r u", g=2, u=2),
                     )
@@ -332,13 +348,15 @@ def tile_diffucoderattention_pa_kernel(tc, hidden_states, Wq_bytes, Wq_scale, Wk
         q_step(0, 2)
         turn_x(1)
         flush(0)
+        banks_v0 = fill_v(0)
         widen(1, 0)
 
         k_acc = {}
         for tt in range(TT):
             k_acc[tt] = matmuls(tt, kc[:, :, :], ks[:, :, :], "A")
 
-        il_v0 = il_v(0)
+        il_v0 = empty_v(banks_v0)
+        banks_v1 = fill_v(1)
         q_step(0, 3)
         widen(1, 1)
 
@@ -350,6 +368,7 @@ def tile_diffucoderattention_pa_kernel(tc, hidden_states, Wq_bytes, Wq_scale, Wk
             copy_on("v" if tt < 2 else "s", heads_of(y_k[tt][:], 128)[:, :, 64:128], heads_of(k_acc[tt][:], 128)[:, :, 64:128])
             nc.sync.dma_start(out=k_out[tt * P : (tt + 1) * P, :], in_=y_k[tt][:])
 
+        il_v1 = empty_v(banks_v1)
         q_step(1, 0)
         widen(1, 2)
 
@@ -372,7 +391,6 @@ def tile_diffucoderattention_pa_kernel(tc, hidden_states, Wq_bytes, Wq_scale, Wk
 
         quantize_v(0, il_v0)
         flush(0)
-        il_v1 = il_v(1)
         widen(1, 3)
 
         q_step(1, 1)

@@ -394,6 +394,7 @@ def tile_diffucoderattention_pa_kernel(tc, hidden_states, Wq_bytes, Wq_scale, Wk
         widen(1, 3)
 
         q_step(1, 1)
+        quantize_v(1, il_v1)
 
         y_q = {}
         for tt in range(TT):
@@ -405,13 +406,24 @@ def tile_diffucoderattention_pa_kernel(tc, hidden_states, Wq_bytes, Wq_scale, Wk
 
         rot_acc = open_group(0, "A")
 
-        quantize_v(1, il_v1)
         v_acc = {}
         for tt in range(TT):
             v_acc[tt] = matmuls(tt, vc[:, :, :], vs[:, :, :], "B")
         q_step(1, 2)
-        q_step(1, 3)
-        flush(0)
+        il_2 = pending[done["pending"]][0]
+        done["pending"] += 1
+        il_3 = il_q(1, 3)
+        for half in range(2):
+            for g, il in ((2, il_2), (3, il_3)):
+                nc.vector.quantize_mx(
+                    out=qc[1][:, g, half * 512 : (half + 1) * 512].bitcast(FP8X4),
+                    scales=qs[1][:, g, half * 512 : (half + 1) * 512],
+                    in_=il[:, half * 2048 : (half + 1) * 2048],
+                )
+                if half == 0:
+                    ready.append(g)
+                    for tt in range(TT):
+                        one_pass(rot_acc[tt][:], tt, g, qc[1][:, :, 0:512], qs[1][:, :, 0:512])
         for tt in range(TT):
             y = xy.tile([P, 512], F32, name="y_v", tag="y_v", bufs=4)
             copy_on("s", y[:], v_acc[tt][:])

@@ -24,12 +24,9 @@ PAIRS = 32
 FREQ_STEP = 10000.0 ** (-1.0 / 32.0)
 TWO_PI_HI = 6.28125
 TWO_PI_LO = 2.0 * math.pi - TWO_PI_HI
-
-SCALAR_Q_HALVES = ((1, 2, 1), (1, 3, 1))
 RUN = 8
-XENG = ("ss", "ss")
-VP = {(0, 3): (0, 1)}
-VECTOR_X_COPIES = ((0, 0), (1, 0), (2, 0), (3, 0))
+ROT = 0
+PLAIN = 1
 
 
 def tile_diffucoderattention_pa_kernel(tc, hidden_states, Wq_bytes, Wq_scale, Wk, Wv, out_0, out_1, out_2):
@@ -53,24 +50,30 @@ def tile_diffucoderattention_pa_kernel(tc, hidden_states, Wq_bytes, Wq_scale, Wk
         psum = ctx.enter_context(tc.psum_pool(name="psum", bufs=4))
 
         scl = const.tile([P, G * PACK], F32, name="scl")
-        nc.sync.dma_start(
-            out=scl[:].rearrange("p (g t) -> p g t", t=PACK),
-            in_=Wq_scale.rearrange("(g p t) o -> p g (t o)", p=P, t=PACK),
-        )
-        wq_bytes = {}
+        plane = {}
         wk_raw = {}
         wv_raw = {}
         x_sb = {}
 
-        def load_q(j, g, th):
-            tl = raw.tile([P, 2, 1024], U8, name="wq_bytes_%d_%d_%d" % (j, g, th))
-            nc.sync.dma_start(out=tl[:], in_=wq_view[g][:, 2 * th : 2 * th + 2, j * 1024 : (j + 1) * 1024])
-            wq_bytes[(j, g, th)] = tl
+        def load_scl():
+            nc.sync.dma_start(
+                out=scl[:].rearrange("p (g t) -> p g t", t=PACK),
+                in_=Wq_scale.rearrange("(g p t) o -> p g (t o)", p=P, t=PACK),
+            )
 
-        def load_k(g):
-            tl = raw.tile([P, PACK, 512], BF16, name="wk_raw", tag="wkv", bufs=4)
-            nc.sync.dma_start(out=tl[:], in_=wk_view[g])
-            wk_raw[g] = tl
+        def load_q(j, g, t0, nt):
+            tl = raw.tile([P, nt, 1024], U8, name="wq_bytes_%d_%d_%d" % (j, g, t0))
+            nc.sync.dma_start(out=tl[:], in_=wq_view[g][:, t0 : t0 + nt, j * 1024 : (j + 1) * 1024])
+            for t in range(nt):
+                plane[(j, g, t0 + t)] = tl[:, t, :]
+
+        def load_k(g, c0=0, c1=512):
+            if c1 - c0 == 512:
+                tl = raw.tile([P, PACK, 512], BF16, name="wk_raw", tag="wkv", bufs=4)
+            else:
+                tl = raw.tile([P, PACK, c1 - c0], BF16, name="wk_part_%d_%d" % (g, c0))
+            nc.sync.dma_start(out=tl[:], in_=wk_view[g][:, :, c0:c1])
+            wk_raw.setdefault(g, []).append((c0, c1, tl))
 
         def load_v(g):
             tl = raw.tile([P, PACK, 512], BF16, name="wv_raw", tag="wkv", bufs=4)
@@ -82,25 +85,26 @@ def tile_diffucoderattention_pa_kernel(tc, hidden_states, Wq_bytes, Wq_scale, Wk
             nc.sync.dma_start(out=tl[:], in_=x_rows[tt * P : (tt + 1) * P, :])
             x_sb[tt] = tl
 
-        load_q(0, 0, 0)
+        load_scl()
+        load_q(0, 0, 0, 2)
         load_k(0)
-        load_q(0, 0, 1)
+        load_q(0, 0, 2, 2)
         load_k(1)
-        load_q(0, 1, 0)
-        load_q(0, 1, 1)
+        load_q(0, 1, 0, 2)
+        load_q(0, 1, 2, 2)
         load_k(2)
         load_k(3)
-        load_q(0, 2, 0)
-        load_q(0, 2, 1)
+        load_q(0, 2, 0, 2)
+        load_q(0, 2, 2, 2)
         load_x(0)
         load_x(1)
-        load_q(0, 3, 0)
-        load_q(0, 3, 1)
+        load_q(0, 3, 0, 2)
+        load_q(0, 3, 2, 2)
         load_x(2)
         load_x(3)
         for j, g in ((1, 0), (1, 1)):
-            load_q(j, g, 0)
-            load_q(j, g, 1)
+            load_q(j, g, 0, 2)
+            load_q(j, g, 2, 2)
 
         warm = const.tile([P, 2], F32, name="warm")
         nc.vector.memset(warm[:], 0.0)
@@ -163,39 +167,80 @@ def tile_diffucoderattention_pa_kernel(tc, hidden_states, Wq_bytes, Wq_scale, Wk
 
         wide = {}
 
-        def widen(j, g):
-            tl = widep.tile([P, PACK, 1024], BF16, name="wide", tag="wide")
-            for t in range(PACK):
-                src = wq_bytes[(j, g, t // 2)][:, t % 2, :].bitcast(FP8)
+        def widen(j, g, planes=(0, 1, 2, 3), eng="s"):
+            if (j, g) not in wide:
+                wide[(j, g)] = widep.tile([P, PACK, 1024], BF16, name="wide", tag="wide")
+            tl = wide[(j, g)]
+            for t in planes:
+                src = plane[(j, g, t)].bitcast(FP8)
                 col = scl[:, PACK * g + t : PACK * g + t + 1]
-                if t in VP.get((j, g), ()):
+                if eng == "v":
                     nc.vector.tensor_scalar(out=tl[:, t, :], in0=src, scalar1=col, scalar2=None, op0=ALU.mult)
                 else:
                     nc.scalar.activation(out=tl[:, t, :], in_=src, func=ACT.Copy, scale=col)
-            wide[(j, g)] = tl
 
-        def il_heads(eng, dst, planes, heads, half):
+        il_of = {}
+
+        def il_q(j, g, half, eng):
+            if (j, g) not in il_of:
+                il_of[(j, g)] = ilp.tile([P, 4096], BF16, name="il", tag="il", align_bytes=64)
+            dst = il_of[(j, g)][:, half * 2048 : (half + 1) * 2048]
             copy_on(
                 eng,
-                dst.rearrange("p (h c i t) -> p h c t i", h=heads, i=RUN, t=PACK),
-                planes.rearrange("p t (h c i) -> p h c t i", h=heads, i=RUN)[:, :, half * (64 // RUN) : (half + 1) * (64 // RUN), :, :],
+                dst.rearrange("p (h c i t) -> p h c t i", h=8, i=RUN, t=PACK),
+                wide[(j, g)][:].rearrange("p t (h c i) -> p h c t i", h=8, i=RUN)[:, :, half * (64 // RUN) : (half + 1) * (64 // RUN), :, :],
             )
 
-        def il_q(j, g):
-            il = ilp.tile([P, 4096], BF16, name="il", tag="il", align_bytes=64)
-            for half in range(2):
-                il_heads("s" if (j, g, half) in SCALAR_Q_HALVES else "v", il[:, half * 2048 : (half + 1) * 2048], wide[(j, g)][:], 8, half)
-            return il
+        def fill_q(j, g, half, side="B"):
+            banks = []
+            for b in range(2):
+                bank = psum.tile([P, 1024], BF16, name="rq", tag=side)
+                for k in range(2):
+                    nc.tensor.matmul(
+                        out=bank[:].rearrange("p (h f t) -> p t h f", h=4, t=PACK)[:, 2 * k : 2 * k + 2, :, :],
+                        lhsT=ident_b[:],
+                        rhs=wide[(j, g)][:, 2 * k : 2 * k + 2, :].rearrange("p t (h f) -> p t h f", f=128)[
+                            :, :, 4 * b : 4 * b + 4, half * 64 : (half + 1) * 64
+                        ],
+                        start=True,
+                        stop=True,
+                    )
+                banks.append(bank)
+            return banks
 
-        def il_k(gp):
-            il = ilp.tile([P, 4096], BF16, name="il", tag="il", align_bytes=64)
-            for gl in range(2):
+        def empty_q(j, g, half, banks, eng="s"):
+            if (j, g) not in il_of:
+                il_of[(j, g)] = ilp.tile([P, 4096], BF16, name="il", tag="il", align_bytes=64)
+            for b in range(2):
+                lo = half * 2048 + b * 1024
+                copy_on(eng, il_of[(j, g)][:, lo : lo + 1024].bitcast(F32), banks[b][:].bitcast(F32))
+
+        def quant_q(j, g, halves=(ROT, PLAIN)):
+            lo = halves[0] * 512
+            hi = (halves[-1] + 1) * 512
+            nc.vector.quantize_mx(out=qc[j][:, g, lo:hi].bitcast(FP8X4), scales=qs[j][:, g, lo:hi], in_=il_of[(j, g)][:, 4 * lo : 4 * hi])
+
+        ilk_of = {}
+
+        def il_k(g, first=0, last=None):
+            gp = g // 2
+            if gp not in ilk_of:
+                ilk_of[gp] = ilp.tile([P, 4096], BF16, name="il", tag="il", align_bytes=64)
+            for c0, c1, tl in wk_raw[g][first:last]:
+                lo = (g % 2) * 2048 + PACK * c0
+                hi = (g % 2) * 2048 + PACK * c1
                 copy_on(
                     "v",
-                    il[:, gl * 2048 : (gl + 1) * 2048].rearrange("p (c i t) -> p c t i", i=RUN, t=PACK),
-                    wk_raw[2 * gp + gl][:].rearrange("p t (c i) -> p c t i", i=RUN),
+                    ilk_of[gp][:, lo:hi].rearrange("p (c i t) -> p c t i", i=RUN, t=PACK),
+                    tl[:].rearrange("p t (c i) -> p c t i", i=RUN),
                 )
-            return il
+
+        def quant_k(gp):
+            nc.vector.quantize_mx(
+                out=kc[:, 2 * gp : 2 * gp + 2, :].rearrange("p g n -> p (g n)").bitcast(FP8X4),
+                scales=ks[:, 2 * gp : 2 * gp + 2, :].rearrange("p g n -> p (g n)"),
+                in_=ilk_of[gp][:],
+            )
 
         def fill_v(gp):
             banks = []
@@ -212,6 +257,30 @@ def tile_diffucoderattention_pa_kernel(tc, hidden_states, Wq_bytes, Wq_scale, Wk
                         )
                     banks.append(bank)
             return banks
+
+        def fill_vg(g, side="B"):
+            banks = []
+            for b in range(2):
+                bank = psum.tile([P, 1024], BF16, name="rt", tag=side)
+                for k in range(2):
+                    nc.tensor.matmul(
+                        out=bank[:].rearrange("p (c t) -> p t c", t=PACK)[:, 2 * k : 2 * k + 2, :],
+                        lhsT=ident_b[:],
+                        rhs=wv_raw[g][:, 2 * k : 2 * k + 2, b * 256 : (b + 1) * 256],
+                        start=True,
+                        stop=True,
+                    )
+                banks.append(bank)
+            return banks
+
+        ilv_of = {}
+
+        def empty_vg(g, banks):
+            if g // 2 not in ilv_of:
+                ilv_of[g // 2] = ilp.tile([P, 4096], BF16, name="ilt", tag="ilt", bufs=2, align_bytes=64)
+            for b in range(2):
+                lo = (g % 2) * 2048 + b * 1024
+                copy_on("s", ilv_of[g // 2][:, lo : lo + 1024].bitcast(F32), banks[b][:].bitcast(F32))
 
         def empty_v(banks):
             il = ilp.tile([P, 4096], BF16, name="ilt", tag="ilt", bufs=2, align_bytes=64)
@@ -231,12 +300,25 @@ def tile_diffucoderattention_pa_kernel(tc, hidden_states, Wq_bytes, Wq_scale, Wk
                 stop=(g == G - 1),
             )
 
-        def matmuls(tt, codes, scales, side):
-            n = codes.shape[2]
-            acc = psum.tile([P, 512], F32, name="acc", tag=side)
-            for g in range(G):
-                one_pass(acc[:, 0:n], tt, g, codes, scales)
-            return acc
+        def banks_of(side):
+            accs = []
+            for tt in range(TT):
+                acc = psum.tile([P, 512], F32, name="acc", tag=side)
+                accs.append(acc)
+            return accs
+
+        def passes(accs, codes, scales, gs=(0, 1, 2, 3), by_bank=True):
+            if by_bank:
+                for tt in range(TT):
+                    for g in gs:
+                        one_pass(accs[tt][:], tt, g, codes, scales)
+            else:
+                for g in gs:
+                    for tt in range(TT):
+                        one_pass(accs[tt][:], tt, g, codes, scales)
+
+        def q_half(j, half):
+            return qc[j][:, :, half * 512 : (half + 1) * 512], qs[j][:, :, half * 512 : (half + 1) * 512]
 
         def heads_of(ap, width):
             return ap.rearrange("p (h f) -> p h f", f=width)
@@ -261,50 +343,17 @@ def tile_diffucoderattention_pa_kernel(tc, hidden_states, Wq_bytes, Wq_scale, Wk
         def rope(tt, rot, y_rot, add_eng):
             rope_sum(rope_products(tt, rot), y_rot, add_eng)
 
-        ctx.enter_context(tc.manual_schedule())
+        xg_of = {}
 
-        pending = []
-        done = {"pending": 0}
-        step_groups = []
-        ready = []
-
-        def open_group(lo, side):
-            accs = []
-            for tt in range(TT):
-                acc1 = psum.tile([P, 512], F32, name="acc1", tag=side)
-                accs.append(acc1)
-            for tt in range(TT):
-                for g in ready:
-                    one_pass(accs[tt][:], tt, g, qc[1][:, :, lo : lo + 512], qs[1][:, :, lo : lo + 512])
-            step_groups.append((lo, accs))
-            return accs
-
-        def run(unit):
-            il, codes, scales, g = unit
-            nc.vector.quantize_mx(out=codes.bitcast(FP8X4), scales=scales, in_=il[:])
-            if g is not None:
-                ready.append(g)
-                for lo, accs in step_groups:
-                    for tt in range(TT):
-                        one_pass(accs[tt][:], tt, g, qc[1][:, :, lo : lo + 512], qs[1][:, :, lo : lo + 512])
-
-        def flush(keep_back):
-            while len(pending) - done["pending"] > keep_back:
-                run(pending[done["pending"]])
-                done["pending"] += 1
-
-        def q_step(j, g):
-            pending.append((il_q(j, g), qc[j][:, g, :], qs[j][:, g, :], g if j == 1 else None))
-            flush(1)
-
-        def turn_x(tp):
+        def turn_x(tp, sides=("A", "B")):
             xg = ilp.tile([P, 4096], BF16, name="xg", tag="il", align_bytes=64)
+            xg_of[tp] = xg
             xg_words = xg[:].bitcast(F32).rearrange("p (a g r u) -> p a g r u", a=2, g=G, u=2)
             for a in range(2):
                 tt = 2 * tp + a
                 words = x_sb[tt][:].bitcast(F32)
                 for gp in range(2):
-                    xt = psum.tile([P, 512], F32, name="xt", tag="A" if gp == 0 else "B")
+                    xt = psum.tile([P, 512], F32, name="xt", tag=sides[gp])
                     for gl in range(2):
                         g = 2 * gp + gl
                         for u in range(2):
@@ -314,50 +363,94 @@ def tile_diffucoderattention_pa_kernel(tc, hidden_states, Wq_bytes, Wq_scale, Wk
                                 ident[:],
                             )
                     copy_on(
-                        XENG[tp][gp],
+                        "s",
                         xg_words[:, a, 2 * gp : 2 * gp + 2, :, :],
                         xt[:].rearrange("p (g u r) -> p g r u", g=2, u=2),
                     )
-            pending.append((xg, xc[tp][:], xs[tp][:], None))
-            flush(1)
 
-        def k_unit(gp):
-            pending.append((
-                il_k(gp),
-                kc[:, 2 * gp : 2 * gp + 2, :].rearrange("p g n -> p (g n)"),
-                ks[:, 2 * gp : 2 * gp + 2, :].rearrange("p g n -> p (g n)"),
-                None,
-            ))
-            flush(1)
+        xt_of = {}
 
+        def turn_x_pe(tp, sides=("A", "B")):
+            for a in range(2):
+                tt = 2 * tp + a
+                words = x_sb[tt][:].bitcast(F32)
+                for gp in range(2):
+                    xt = psum.tile([P, 512], F32, name="xt", tag=sides[gp])
+                    xt_of[(tt, gp)] = xt
+                    for gl in range(2):
+                        g = 2 * gp + gl
+                        for u in range(2):
+                            nc.tensor.transpose(
+                                xt[:, (2 * gl + u) * P : (2 * gl + u + 1) * P],
+                                words[:, 256 * g + u : 256 * (g + 1) : 2],
+                                ident[:],
+                            )
+
+        def turn_x_out(tp):
+            xg = ilp.tile([P, 4096], BF16, name="xg", tag="il", align_bytes=64)
+            xg_of[tp] = xg
+            xg_words = xg[:].bitcast(F32).rearrange("p (a g r u) -> p a g r u", a=2, g=G, u=2)
+            for a in range(2):
+                for gp in range(2):
+                    copy_on(
+                        "s",
+                        xg_words[:, a, 2 * gp : 2 * gp + 2, :, :],
+                        xt_of[(2 * tp + a, gp)][:].rearrange("p (g u r) -> p g r u", g=2, u=2),
+                    )
+
+        def quant_x(tp):
+            nc.vector.quantize_mx(out=xc[tp][:].bitcast(FP8X4), scales=xs[tp][:], in_=xg_of[tp][:])
+
+        vcs = {}
+
+        def quant_v(gp, il):
+            if "c" not in vcs:
+                vcs["c"] = keep.tile([P, G, 512], U32, name="vc", tag="kvc", align_bytes=64)
+                vcs["s"] = keep.tile([P, G, 512], U8, name="vs", tag="kvs", align_bytes=64)
+            nc.vector.quantize_mx(
+                out=vcs["c"][:, 2 * gp : 2 * gp + 2, :].rearrange("p g n -> p (g n)").bitcast(FP8X4),
+                scales=vcs["s"][:, 2 * gp : 2 * gp + 2, :].rearrange("p g n -> p (g n)"),
+                in_=il[:],
+            )
+
+        ctx.enter_context(tc.manual_schedule())
         widen(0, 0)
         widen(0, 1)
-        k_unit(0)
-        flush(0)
-        q_step(0, 0)
-        k_unit(1)
+        il_k(0)
+        il_k(1)
+        quant_k(0)
+        il_q(0, 0, ROT, "v")
+        il_q(0, 0, PLAIN, "v")
+        il_k(2)
+        il_k(3)
+        quant_q(0, 0)
         for g in range(G):
             load_v(g)
         for g in (2, 3):
-            load_q(1, g, 0)
-            load_q(1, g, 1)
+            load_q(1, g, 0, 2)
+            load_q(1, g, 2, 2)
         widen(0, 2)
-        q_step(0, 1)
+        il_q(0, 1, ROT, "v")
+        il_q(0, 1, PLAIN, "v")
+        quant_k(1)
         turn_x(0)
-        widen(0, 3)
-        q_step(0, 2)
+        quant_q(0, 1)
+        widen(0, 3, (0, 1), "v")
+        widen(0, 3, (2, 3), "s")
+        il_q(0, 2, ROT, "v")
+        il_q(0, 2, PLAIN, "v")
+        quant_x(0)
         turn_x(1)
-        flush(0)
+        quant_q(0, 2)
+        quant_x(1)
         banks_v0 = fill_v(0)
         widen(1, 0)
-
-        k_acc = {}
-        for tt in range(TT):
-            k_acc[tt] = matmuls(tt, kc[:, :, :], ks[:, :, :], "A")
-
+        k_acc = banks_of("A")
+        passes(k_acc, kc[:, :, :], ks[:, :, :])
         il_v0 = empty_v(banks_v0)
         banks_v1 = fill_v(1)
-        q_step(0, 3)
+        il_q(0, 3, ROT, "v")
+        il_q(0, 3, PLAIN, "v")
         widen(1, 1)
 
         y_k = {}
@@ -369,32 +462,20 @@ def tile_diffucoderattention_pa_kernel(tc, hidden_states, Wq_bytes, Wq_scale, Wk
             nc.sync.dma_start(out=k_out[tt * P : (tt + 1) * P, :], in_=y_k[tt][:])
 
         il_v1 = empty_v(banks_v1)
-        q_step(1, 0)
+        il_q(1, 0, ROT, "v")
+        il_q(1, 0, PLAIN, "v")
+        quant_q(0, 3)
         widen(1, 2)
-
-        q_r = {}
-        q_p = {}
-        for tt in range(TT):
-            q_r[tt] = matmuls(tt, qc[0][:, :, 0:512], qs[0][:, :, 0:512], "A")
-        for tt in range(TT):
-            q_p[tt] = matmuls(tt, qc[0][:, :, 512:1024], qs[0][:, :, 512:1024], "B")
-
-        vc = keep.tile([P, G, 512], U32, name="vc", tag="kvc", align_bytes=64)
-        vs = keep.tile([P, G, 512], U8, name="vs", tag="kvs", align_bytes=64)
-
-        def quantize_v(gp, il):
-            nc.vector.quantize_mx(
-                out=vc[:, 2 * gp : 2 * gp + 2, :].rearrange("p g n -> p (g n)").bitcast(FP8X4),
-                scales=vs[:, 2 * gp : 2 * gp + 2, :].rearrange("p g n -> p (g n)"),
-                in_=il[:],
-            )
-
-        quantize_v(0, il_v0)
-        flush(0)
+        q_r = banks_of("A")
+        passes(q_r, *q_half(0, ROT))
+        q_p = banks_of("B")
+        passes(q_p, *q_half(0, PLAIN))
+        quant_v(0, il_v0)
+        quant_q(1, 0)
         widen(1, 3)
-
-        q_step(1, 1)
-        quantize_v(1, il_v1)
+        il_q(1, 1, ROT, "v")
+        il_q(1, 1, PLAIN, "v")
+        quant_v(1, il_v1)
 
         y_q = {}
         for tt in range(TT):
@@ -404,31 +485,30 @@ def tile_diffucoderattention_pa_kernel(tc, hidden_states, Wq_bytes, Wq_scale, Wk
             copy_on("v", heads_of(y_q[tt][:], 128)[:, :, 64:128], heads_of(q_p[tt][:], 64))
             nc.sync.dma_start(out=q_out[tt * P : (tt + 1) * P, 0:1024], in_=y_q[tt][:])
 
-        rot_acc = open_group(0, "A")
+        v_acc = banks_of("A")
+        passes(v_acc, vcs["c"][:, :, :], vcs["s"][:, :, :])
+        rot_acc = banks_of("B")
+        passes(rot_acc, *q_half(1, ROT), gs=(0,))
+        il_q(1, 2, ROT, "v")
+        il_q(1, 2, PLAIN, "s")
+        quant_q(1, 1)
+        passes(rot_acc, *q_half(1, ROT), gs=(1,))
+        il_q(1, 3, ROT, "v")
+        il_q(1, 3, PLAIN, "s")
+        quant_q(1, 2, (ROT,))
+        passes(rot_acc, *q_half(1, ROT), gs=(2,))
+        quant_q(1, 3, (ROT,))
+        passes(rot_acc, *q_half(1, ROT), gs=(3,))
+        quant_q(1, 2, (PLAIN,))
+        quant_q(1, 3, (PLAIN,))
 
-        v_acc = {}
-        for tt in range(TT):
-            v_acc[tt] = matmuls(tt, vc[:, :, :], vs[:, :, :], "B")
-        q_step(1, 2)
-        il_2 = pending[done["pending"]][0]
-        done["pending"] += 1
-        il_3 = il_q(1, 3)
-        for half in range(2):
-            for g, il in ((2, il_2), (3, il_3)):
-                nc.vector.quantize_mx(
-                    out=qc[1][:, g, half * 512 : (half + 1) * 512].bitcast(FP8X4),
-                    scales=qs[1][:, g, half * 512 : (half + 1) * 512],
-                    in_=il[:, half * 2048 : (half + 1) * 2048],
-                )
-                if half == 0:
-                    ready.append(g)
-                    for tt in range(TT):
-                        one_pass(rot_acc[tt][:], tt, g, qc[1][:, :, 0:512], qs[1][:, :, 0:512])
         for tt in range(TT):
             y = xy.tile([P, 512], F32, name="y_v", tag="y_v", bufs=4)
             copy_on("s", y[:], v_acc[tt][:])
             nc.sync.dma_start(out=v_out[tt * P : (tt + 1) * P, :], in_=y[:])
-        plain_acc = open_group(512, "B")
+
+        plain_acc = banks_of("A")
+        passes(plain_acc, *q_half(1, PLAIN))
 
         for tt in range(TT):
             y_q[tt] = xy.tile([P, 1024], F32, name="y_q", tag="xy")

@@ -462,9 +462,9 @@ def tile_diffucoderattention_pa_kernel(tc, hidden_states, Wq_bytes, Wq_scale, Wk
             nc.sync.dma_start(out=k_out[tt * P : (tt + 1) * P, :], in_=y_k[tt][:])
 
         il_v1 = empty_v(banks_v1)
+        quant_q(0, 3)
         il_q(1, 0, ROT, "v")
         il_q(1, 0, PLAIN, "v")
-        quant_q(0, 3)
         widen(1, 2)
         q_r = banks_of("A")
         passes(q_r, *q_half(0, ROT))
@@ -476,6 +476,7 @@ def tile_diffucoderattention_pa_kernel(tc, hidden_states, Wq_bytes, Wq_scale, Wk
         il_q(1, 1, ROT, "v")
         il_q(1, 1, PLAIN, "v")
         quant_v(1, il_v1)
+        quant_q(1, 1)
 
         y_q = {}
         for tt in range(TT):
@@ -488,12 +489,20 @@ def tile_diffucoderattention_pa_kernel(tc, hidden_states, Wq_bytes, Wq_scale, Wk
         v_acc = banks_of("A")
         passes(v_acc, vcs["c"][:, :, :], vcs["s"][:, :, :])
         rot_acc = banks_of("B")
-        passes(rot_acc, *q_half(1, ROT), gs=(0,))
+        passes(rot_acc, *q_half(1, ROT), gs=(0, 1))
+
         il_q(1, 2, ROT, "v")
         il_q(1, 2, PLAIN, "s")
-        quant_q(1, 1)
-        passes(rot_acc, *q_half(1, ROT), gs=(1,))
         il_q(1, 3, ROT, "v")
+        plain_acc = {}
+        for tt in range(2):
+            y = xy.tile([P, 512], F32, name="y_v", tag="y_v", bufs=4)
+            copy_on("s", y[:], v_acc[tt][:])
+            nc.sync.dma_start(out=v_out[tt * P : (tt + 1) * P, :], in_=y[:])
+        for tt in range(2):
+            plain_acc[tt] = psum.tile([P, 512], F32, name="acc", tag="A")
+            for g in (0, 1):
+                one_pass(plain_acc[tt][:], tt, g, *q_half(1, PLAIN))
         il_q(1, 3, PLAIN, "s")
         quant_q(1, 2, (ROT,))
         passes(rot_acc, *q_half(1, ROT), gs=(2,))
@@ -501,14 +510,17 @@ def tile_diffucoderattention_pa_kernel(tc, hidden_states, Wq_bytes, Wq_scale, Wk
         passes(rot_acc, *q_half(1, ROT), gs=(3,))
         quant_q(1, 2, (PLAIN,))
         quant_q(1, 3, (PLAIN,))
-
-        for tt in range(TT):
+        for tt in range(2, TT):
             y = xy.tile([P, 512], F32, name="y_v", tag="y_v", bufs=4)
             copy_on("s", y[:], v_acc[tt][:])
             nc.sync.dma_start(out=v_out[tt * P : (tt + 1) * P, :], in_=y[:])
-
-        plain_acc = banks_of("A")
-        passes(plain_acc, *q_half(1, PLAIN))
+        for tt in range(2):
+            for g in (2, 3):
+                one_pass(plain_acc[tt][:], tt, g, *q_half(1, PLAIN))
+        for tt in range(2, TT):
+            plain_acc[tt] = psum.tile([P, 512], F32, name="acc", tag="A")
+            for g in range(G):
+                one_pass(plain_acc[tt][:], tt, g, *q_half(1, PLAIN))
 
         for tt in range(TT):
             y_q[tt] = xy.tile([P, 1024], F32, name="y_q", tag="xy")

@@ -414,7 +414,8 @@ def tile_diffucoderattention_pa_kernel(tc, hidden_states, Wq_bytes, Wq_scale, Wk
             )
 
         ctx.enter_context(tc.manual_schedule())
-        widen(0, 0)
+        widen(0, 0, (1,), "v")
+        widen(0, 0, (0, 2, 3), "s")
         widen(0, 1)
         il_k(0)
         il_k(1)
@@ -435,8 +436,8 @@ def tile_diffucoderattention_pa_kernel(tc, hidden_states, Wq_bytes, Wq_scale, Wk
         quant_k(1)
         turn_x(0)
         quant_q(0, 1)
-        widen(0, 3, (0, 1), "v")
-        widen(0, 3, (2, 3), "s")
+        widen(0, 3, (0,), "v")
+        widen(0, 3, (1, 2, 3), "s")
         il_q(0, 2, ROT, "v")
         il_q(0, 2, PLAIN, "v")
         quant_x(0)

@@ -323,10 +323,19 @@ def tile_diffucoderattention_pa_kernel(tc, hidden_states, Wq_bytes, Wq_scale, Wk
         def heads_of(ap, width):
             return ap.rearrange("p (h f) -> p h f", f=width)
 
-        def rope_products(tt, rot):
+        def rope_products(tt, rot, both=True):
             heads = rot.shape[1]
             n = heads * 64
             z = zp.tile([P, 2, 512], F32, name="z", tag="z")
+            if both:
+                shape = [P, 2, heads, PAIRS, 2]
+                nc.vector.tensor_tensor(
+                    out=z[:, :, 0:n].rearrange("p r (h i e) -> p r h i e", h=heads, e=2),
+                    in0=rot.rearrange("p h (i r) -> p r h i", r=2).unsqueeze(4).to_broadcast(shape),
+                    in1=tab[:, tt, :, :, :].unsqueeze(2).to_broadcast(shape),
+                    op=ALU.mult,
+                )
+                return z[:, :, 0:n]
             shape = [P, heads, PAIRS, 2]
             for r in range(2):
                 nc.vector.tensor_tensor(
@@ -340,8 +349,8 @@ def tile_diffucoderattention_pa_kernel(tc, hidden_states, Wq_bytes, Wq_scale, Wk
         def rope_sum(z, y_rot, add_eng):
             add_eng.tensor_tensor(out=y_rot, in0=heads_of(z[:, 0, :], 64), in1=heads_of(z[:, 1, :], 64), op=ALU.add)
 
-        def rope(tt, rot, y_rot, add_eng):
-            rope_sum(rope_products(tt, rot), y_rot, add_eng)
+        def rope(tt, rot, y_rot, add_eng, both=True):
+            rope_sum(rope_products(tt, rot, both), y_rot, add_eng)
 
         xg_of = {}
 
@@ -457,7 +466,7 @@ def tile_diffucoderattention_pa_kernel(tc, hidden_states, Wq_bytes, Wq_scale, Wk
         y_k = {}
         for tt in range(TT):
             y_k[tt] = xy.tile([P, 512], F32, name="y_k", tag="xy")
-            rope(tt, heads_of(k_acc[tt][:], 128)[:, :, 0:64], heads_of(y_k[tt][:], 128)[:, :, 0:64], nc.gpsimd)
+            rope(tt, heads_of(k_acc[tt][:], 128)[:, :, 0:64], heads_of(y_k[tt][:], 128)[:, :, 0:64], nc.gpsimd, False)
         for tt in range(TT):
             copy_on("v" if tt < 2 else "s", heads_of(y_k[tt][:], 128)[:, :, 64:128], heads_of(k_acc[tt][:], 128)[:, :, 64:128])
             nc.sync.dma_start(out=k_out[tt * P : (tt + 1) * P, :], in_=y_k[tt][:])

@@ -56,7 +56,7 @@ def tile_diffucoderattention_pa_kernel(tc, hidden_states, Wq_bytes, Wq_scale, Wk
         x_sb = {}
 
         def load_scl():
-            nc.sync.dma_start(
+            nc.scalar.dma_start(
                 out=scl[:].rearrange("p (g t) -> p g t", t=PACK),
                 in_=Wq_scale.rearrange("(g p t) o -> p g (t o)", p=P, t=PACK),
             )

@@ -149,15 +149,15 @@ def tile_diffucoderattention_pa_kernel(tc, hidden_states, Wq_bytes, Wq_scale, Wk
         xc = {}
         xs = {}
         for tp in range(2):
-            xc[tp] = keep.tile([P, 2 * G * P], U32, name="xc_%d" % tp, align_bytes=64)
-            xs[tp] = keep.tile([P, 2 * G * P], U8, name="xs_%d" % tp, align_bytes=64)
+            xc[tp] = keep.tile([P, 2 * G * P], U32, name="xc_%d" % tp, align_bytes=256)
+            xs[tp] = keep.tile([P, 2 * G * P], U8, name="xs_%d" % tp, align_bytes=256)
         qc = {}
         qs = {}
         for j in range(2):
-            qc[j] = keep.tile([P, G, 1024], U32, name="qc_%d" % j, align_bytes=64)
-            qs[j] = keep.tile([P, G, 1024], U8, name="qs_%d" % j, align_bytes=64)
-        kc = keep.tile([P, G, 512], U32, name="kc", tag="kvc", align_bytes=64)
-        ks = keep.tile([P, G, 512], U8, name="ks", tag="kvs", align_bytes=64)
+            qc[j] = keep.tile([P, G, 1024], U32, name="qc_%d" % j, align_bytes=256)
+            qs[j] = keep.tile([P, G, 1024], U8, name="qs_%d" % j, align_bytes=256)
+        kc = keep.tile([P, G, 512], U32, name="kc", tag="kvc", align_bytes=256)
+        ks = keep.tile([P, G, 512], U8, name="ks", tag="kvs", align_bytes=256)
 
         def copy_on(eng, out, in_):
             if eng == "v":
@@ -414,8 +414,8 @@ def tile_diffucoderattention_pa_kernel(tc, hidden_states, Wq_bytes, Wq_scale, Wk
 
         def quant_v(gp, il):
             if "c" not in vcs:
-                vcs["c"] = keep.tile([P, G, 512], U32, name="vc", tag="kvc", align_bytes=64)
-                vcs["s"] = keep.tile([P, G, 512], U8, name="vs", tag="kvs", align_bytes=64)
+                vcs["c"] = keep.tile([P, G, 512], U32, name="vc", tag="kvc", align_bytes=256)
+                vcs["s"] = keep.tile([P, G, 512], U8, name="vs", tag="kvs", align_bytes=256)
             nc.vector.quantize_mx(
                 out=vcs["c"][:, 2 * gp : 2 * gp + 2, :].rearrange("p g n -> p (g n)").bitcast(FP8X4),
                 scales=vcs["s"][:, 2 * gp : 2 * gp + 2, :].rearrange("p g n -> p (g n)"),

@@ -140,11 +140,10 @@ def tile_diffucoderattention_pa_kernel(tc, hidden_states, Wq_bytes, Wq_scale, Wk
         nc.vector.scalar_tensor_tensor(out=mag[:], in0=red[:], scalar=-1.0, in1=red[:], op0=ALU.mult, op1=ALU.max)
         red3 = red[:].rearrange("p (t i) -> p t i", i=PAIRS)
         mag3 = mag[:].rearrange("p (t i) -> p t i", i=PAIRS)
-        tab = const.tile([P, TT, 2, PAIRS, 2], F32, name="tab")
-        nc.scalar.activation(out=tab[:, :, 0, :, 1], in_=red3, func=ACT.Sin)
-        nc.scalar.activation(out=tab[:, :, 1, :, 0], in_=red3, func=ACT.Sin, scale=-1.0)
-        nc.scalar.activation(out=tab[:, :, 0, :, 0], in_=mag3, func=ACT.Sin, scale=-1.0, bias=math.pi / 2.0)
-        nc.scalar.activation(out=tab[:, :, 1, :, 1], in_=mag3, func=ACT.Sin, scale=-1.0, bias=math.pi / 2.0)
+        tab = const.tile([P, 3, TT, PAIRS], F32, name="tab")
+        nc.scalar.activation(out=tab[:, 0, :, :], in_=red3, func=ACT.Sin, scale=-1.0)
+        nc.scalar.activation(out=tab[:, 2, :, :], in_=red3, func=ACT.Sin)
+        nc.scalar.activation(out=tab[:, 1, :, :], in_=mag3, func=ACT.Sin, scale=-1.0, bias=math.pi / 2.0)
 
         xc = {}
         xs = {}
@@ -327,21 +326,12 @@ def tile_diffucoderattention_pa_kernel(tc, hidden_states, Wq_bytes, Wq_scale, Wk
             heads = rot.shape[1]
             n = heads * 64
             z = zp.tile([P, 2, 512], F32, name="z", tag="z")
-            if both:
-                shape = [P, 2, heads, PAIRS, 2]
-                nc.vector.tensor_tensor(
-                    out=z[:, :, 0:n].rearrange("p r (h i e) -> p r h i e", h=heads, e=2),
-                    in0=rot.rearrange("p h (i r) -> p r h i", r=2).unsqueeze(4).to_broadcast(shape),
-                    in1=tab[:, tt, :, :, :].unsqueeze(2).to_broadcast(shape),
-                    op=ALU.mult,
-                )
-                return z[:, :, 0:n]
             shape = [P, heads, PAIRS, 2]
             for r in range(2):
                 nc.vector.tensor_tensor(
                     out=z[:, r, 0:n].rearrange("p (h i e) -> p h i e", h=heads, e=2),
                     in0=rot.rearrange("p h (i e) -> p h i e", e=2)[:, :, :, r : r + 1].to_broadcast(shape),
-                    in1=tab[:, tt, r, :, :].unsqueeze(1).to_broadcast(shape),
+                    in1=tab[:, 1 - r : 3 - r, tt, :].rearrange("p e i -> p i e").unsqueeze(1).to_broadcast(shape),
                     op=ALU.mult,
                 )
             return z[:, :, 0:n]

@@ -2,7 +2,6 @@ import math
 from contextlib import ExitStack
 
 import concourse.mybir as mybir
-from concourse.masks import make_identity
 
 FLOPS = 2 * 512 * 2048 * 3072
 
@@ -22,8 +21,6 @@ TT = 4
 G = 4
 PAIRS = 32
 FREQ_STEP = 10000.0 ** (-1.0 / 32.0)
-TWO_PI_HI = 6.28125
-TWO_PI_LO = 2.0 * math.pi - TWO_PI_HI
 RUN = 8
 ROT = 0
 PLAIN = 1
@@ -48,6 +45,8 @@ def tile_diffucoderattention_pa_kernel(tc, hidden_states, Wq_bytes, Wq_scale, Wk
         ilp = ctx.enter_context(tc.tile_pool(name="ilp", bufs=3))
         zp = ctx.enter_context(tc.tile_pool(name="zp", bufs=3))
         psum = ctx.enter_context(tc.psum_pool(name="psum", bufs=4))
+
+        ctx.enter_context(tc.manual_schedule())
 
         scl = const.tile([P, G * PACK], F32, name="scl")
         plane = {}
@@ -110,40 +109,40 @@ def tile_diffucoderattention_pa_kernel(tc, hidden_states, Wq_bytes, Wq_scale, Wk
         nc.vector.memset(warm[:], 0.0)
         nc.scalar.activation(out=warm[:, 1:2], in_=warm[:, 0:1], func=ACT.Sin)
 
-        ident = const.tile([P, P], F32, name="ident")
-        make_identity(nc, ident[:])
-        ident_b = const.tile([P, P], BF16, name="ident_b")
-        make_identity(nc, ident_b[:])
+        turns = const.tile([P, TT, PAIRS], F32, name="turns")
+        nc.gpsimd.iota(
+            turns[:].rearrange("p t i -> p (t i)"), pattern=[[P, TT], [0, PAIRS]], base=0, channel_multiplier=1,
+            allow_small_or_imprecise_dtypes=True,
+        )
+        diag = const.tile([P, P], F32, name="diag")
+        nc.gpsimd.iota(diag[:], pattern=[[-1, P]], base=0, channel_multiplier=1, allow_small_or_imprecise_dtypes=True)
 
-        pos = const.tile([P, TT], F32, name="pos")
-        nc.gpsimd.iota(pos[:], pattern=[[P, TT]], base=0, channel_multiplier=1, allow_small_or_imprecise_dtypes=True)
-        ang = const.tile([P, TT, PAIRS], F32, name="ang")
-        nc.vector.tensor_copy(out=ang[:, :, 0:1], in_=pos[:].unsqueeze(2))
-        for w in (1, 2, 4, 8, 16):
+        by_ab = turns[:].rearrange("p t (a b) -> p t a b", b=8)
+        for a in range(4):
             nc.vector.tensor_scalar(
-                out=ang[:, :, w : 2 * w], in0=ang[:, :, 0:w], scalar1=FREQ_STEP**w, scalar2=None, op0=ALU.mult
+                out=by_ab[:, :, a, :], in0=by_ab[:, :, a, :], scalar1=FREQ_STEP ** (8 * a) / (2.0 * math.pi), scalar2=None, op0=ALU.mult
             )
-        ang_flat = ang[:].rearrange("p t i -> p (t i)")
-        turns_i = const.tile([P, TT * PAIRS], I32, name="turns_i")
-        nc.vector.tensor_scalar(out=turns_i[:], in0=ang_flat, scalar1=1.0 / (2.0 * math.pi), scalar2=None, op0=ALU.mult)
-        turns = const.tile([P, TT * PAIRS], F32, name="turns")
-        nc.vector.tensor_copy(out=turns[:], in_=turns_i[:])
-        red1 = const.tile([P, TT * PAIRS], F32, name="red1")
-        nc.vector.scalar_tensor_tensor(out=red1[:], in0=turns[:], scalar=-TWO_PI_HI, in1=ang_flat, op0=ALU.mult, op1=ALU.add)
-        red2 = const.tile([P, TT * PAIRS], F32, name="red2")
-        nc.vector.scalar_tensor_tensor(out=red2[:], in0=turns[:], scalar=-TWO_PI_LO, in1=red1[:], op0=ALU.mult, op1=ALU.add)
-        wrap = const.tile([P, TT * PAIRS], F32, name="wrap")
-        nc.vector.tensor_scalar(out=wrap[:], in0=red2[:], scalar1=math.pi, scalar2=-2.0 * math.pi, op0=ALU.is_gt, op1=ALU.mult)
-        red = const.tile([P, TT * PAIRS], F32, name="red")
-        nc.vector.tensor_tensor(out=red[:], in0=red2[:], in1=wrap[:], op=ALU.add)
-        mag = const.tile([P, TT * PAIRS], F32, name="mag")
-        nc.vector.scalar_tensor_tensor(out=mag[:], in0=red[:], scalar=-1.0, in1=red[:], op0=ALU.mult, op1=ALU.max)
-        red3 = red[:].rearrange("p (t i) -> p t i", i=PAIRS)
-        mag3 = mag[:].rearrange("p (t i) -> p t i", i=PAIRS)
+        for b in range(1, 8):
+            nc.vector.tensor_scalar(out=by_ab[:, :, :, b], in0=by_ab[:, :, :, b], scalar1=FREQ_STEP**b, scalar2=None, op0=ALU.mult)
+        ident = const.tile([P, P], F32, name="ident")
+        nc.vector.tensor_scalar(out=ident[:], in0=diag[:], scalar1=0.0, scalar2=None, op0=ALU.is_equal)
+        turns_flat = turns[:].rearrange("p t i -> p (t i)")
+        whole = const.tile([P, TT * PAIRS], I32, name="whole")
+        nc.vector.tensor_copy(out=whole[:], in_=turns_flat)
+        ident_b = const.tile([P, P], BF16, name="ident_b")
+        nc.vector.tensor_scalar(out=ident_b[:], in0=diag[:], scalar1=0.0, scalar2=None, op0=ALU.is_equal)
+        frac = const.tile([P, TT * PAIRS], F32, name="frac")
+        nc.vector.tensor_tensor(out=frac[:], in0=turns_flat, in1=whole[:], op=ALU.subtract)
+        afrac = const.tile([P, TT * PAIRS], F32, name="afrac")
+        nc.vector.scalar_tensor_tensor(out=afrac[:], in0=frac[:], scalar=-1.0, in1=frac[:], op0=ALU.mult, op1=ALU.max)
+        frac3 = frac[:].rearrange("p (t i) -> p t i", i=PAIRS)
+        afrac3 = afrac[:].rearrange("p (t i) -> p t i", i=PAIRS)
         tab = const.tile([P, 3, TT, PAIRS], F32, name="tab")
-        nc.scalar.activation(out=tab[:, 0, :, :], in_=red3, func=ACT.Sin, scale=-1.0)
-        nc.scalar.activation(out=tab[:, 2, :, :], in_=red3, func=ACT.Sin)
-        nc.scalar.activation(out=tab[:, 1, :, :], in_=mag3, func=ACT.Sin, scale=-1.0, bias=math.pi / 2.0)
+
+        def make_tables():
+            nc.scalar.activation(out=tab[:, 0, :, :], in_=frac3, func=ACT.Sin, scale=-2.0 * math.pi)
+            nc.scalar.activation(out=tab[:, 2, :, :], in_=frac3, func=ACT.Sin, scale=2.0 * math.pi)
+            nc.scalar.activation(out=tab[:, 1, :, :], in_=afrac3, func=ACT.Sin, scale=-2.0 * math.pi, bias=math.pi / 2.0)
 
         xc = {}
         xs = {}
@@ -412,9 +411,10 @@ def tile_diffucoderattention_pa_kernel(tc, hidden_states, Wq_bytes, Wq_scale, Wk
                 in_=il[:],
             )
 
-        ctx.enter_context(tc.manual_schedule())
         widen(0, 0, (1,), "v")
-        widen(0, 0, (0, 2, 3), "s")
+        widen(0, 0, (0,), "s")
+        make_tables()
+        widen(0, 0, (2, 3), "s")
         widen(0, 1)
         il_k(0)
         il_k(1)

@@ -22,6 +22,7 @@ G = 4
 PAIRS = 32
 FREQ_STEP = 10000.0 ** (-1.0 / 32.0)
 RUN = 8
+PAD_COLUMNS = 392
 ROT = 0
 PLAIN = 1
 
@@ -105,8 +106,8 @@ def tile_diffucoderattention_pa_kernel(tc, hidden_states, Wq_bytes, Wq_scale, Wk
             load_q(j, g, 0, 2)
             load_q(j, g, 2, 2)
 
-        warm = const.tile([P, 2], F32, name="warm")
-        nc.vector.memset(warm[:], 0.0)
+        warm = const.tile([P, 2 + PAD_COLUMNS], F32, name="warm")
+        nc.vector.memset(warm[:, 0:2], 0.0)
         nc.scalar.activation(out=warm[:, 1:2], in_=warm[:, 0:1], func=ACT.Sin)
 
         turns = const.tile([P, TT, PAIRS], F32, name="turns")
@@ -481,9 +482,16 @@ def tile_diffucoderattention_pa_kernel(tc, hidden_states, Wq_bytes, Wq_scale, Wk
         y_q = {}
         for tt in range(TT):
             y_q[tt] = xy.tile([P, 1024], F32, name="y_q", tag="xy")
-            rope(tt, heads_of(q_r[tt][:], 64), heads_of(y_q[tt][:], 128)[:, :, 0:64], nc.gpsimd)
-        for tt in range(TT):
+            if tt < TT - 1:
+                rope(tt, heads_of(q_r[tt][:], 64), heads_of(y_q[tt][:], 128)[:, :, 0:64], nc.gpsimd)
+            else:
+                z_last = rope_products(tt, heads_of(q_r[tt][:], 64))
+        for tt in range(2):
             copy_on("v", heads_of(y_q[tt][:], 128)[:, :, 64:128], heads_of(q_p[tt][:], 64))
+            nc.sync.dma_start(out=q_out[tt * P : (tt + 1) * P, 0:1024], in_=y_q[tt][:])
+        rope_sum(z_last, heads_of(y_q[TT - 1][:], 128)[:, :, 0:64], nc.vector)
+        for tt in range(2, TT):
+            copy_on("s", heads_of(y_q[tt][:], 128)[:, :, 64:128], heads_of(q_p[tt][:], 64))
             nc.sync.dma_start(out=q_out[tt * P : (tt + 1) * P, 0:1024], in_=y_q[tt][:])
 
         v_acc = banks_of("A")
@@ -494,15 +502,6 @@ def tile_diffucoderattention_pa_kernel(tc, hidden_states, Wq_bytes, Wq_scale, Wk
         il_q(1, 2, ROT, "v")
         il_q(1, 2, PLAIN, "s")
         il_q(1, 3, ROT, "v")
-        plain_acc = {}
-        for tt in range(2):
-            y = xy.tile([P, 512], F32, name="y_v", tag="y_v", bufs=4)
-            copy_on("s", y[:], v_acc[tt][:])
-            nc.sync.dma_start(out=v_out[tt * P : (tt + 1) * P, :], in_=y[:])
-        for tt in range(2):
-            plain_acc[tt] = psum.tile([P, 512], F32, name="acc", tag="A")
-            for g in (0, 1):
-                one_pass(plain_acc[tt][:], tt, g, *q_half(1, PLAIN))
         il_q(1, 3, PLAIN, "s")
         quant_q(1, 2, (ROT,))
         passes(rot_acc, *q_half(1, ROT), gs=(2,))
@@ -510,14 +509,12 @@ def tile_diffucoderattention_pa_kernel(tc, hidden_states, Wq_bytes, Wq_scale, Wk
         passes(rot_acc, *q_half(1, ROT), gs=(3,))
         quant_q(1, 2, (PLAIN,))
         quant_q(1, 3, (PLAIN,))
-        for tt in range(2, TT):
+        plain_acc = {}
+        for tt in range(TT):
             y = xy.tile([P, 512], F32, name="y_v", tag="y_v", bufs=4)
             copy_on("s", y[:], v_acc[tt][:])
             nc.sync.dma_start(out=v_out[tt * P : (tt + 1) * P, :], in_=y[:])
-        for tt in range(2):
-            for g in (2, 3):
-                one_pass(plain_acc[tt][:], tt, g, *q_half(1, PLAIN))
-        for tt in range(2, TT):
+        for tt in range(TT):
             plain_acc[tt] = psum.tile([P, 512], F32, name="acc", tag="A")
             for g in range(G):
                 one_pass(plain_acc[tt][:], tt, g, *q_half(1, PLAIN))

@@ -87,19 +87,19 @@ def tile_diffucoderattention_pa_kernel(tc, hidden_states, Wq_bytes, Wq_scale, Wk
 
         load_scl()
         load_q(0, 0, 0, 2)
-        load_k(0)
         load_q(0, 0, 2, 2)
-        load_k(1)
         load_q(0, 1, 0, 2)
         load_q(0, 1, 2, 2)
-        load_k(2)
-        load_k(3)
+        load_k(0)
         load_q(0, 2, 0, 2)
         load_q(0, 2, 2, 2)
+        load_k(1)
         load_x(0)
         load_x(1)
         load_q(0, 3, 0, 2)
         load_q(0, 3, 2, 2)
+        load_k(2)
+        load_k(3)
         load_x(2)
         load_x(3)
         for j, g in ((1, 0), (1, 1)):
@@ -221,7 +221,7 @@ def tile_diffucoderattention_pa_kernel(tc, hidden_states, Wq_bytes, Wq_scale, Wk
 
         ilk_of = {}
 
-        def il_k(g, first=0, last=None):
+        def il_k(g, first=0, last=None, eng="v"):
             gp = g // 2
             if gp not in ilk_of:
                 ilk_of[gp] = ilp.tile([P, 4096], BF16, name="il", tag="il", align_bytes=64)
@@ -229,7 +229,7 @@ def tile_diffucoderattention_pa_kernel(tc, hidden_states, Wq_bytes, Wq_scale, Wk
                 lo = (g % 2) * 2048 + PACK * c0
                 hi = (g % 2) * 2048 + PACK * c1
                 copy_on(
-                    "v",
+                    eng,
                     ilk_of[gp][:, lo:hi].rearrange("p (c i t) -> p c t i", i=RUN, t=PACK),
                     tl[:].rearrange("p t (c i) -> p c t i", i=RUN),
                 )
@@ -412,37 +412,36 @@ def tile_diffucoderattention_pa_kernel(tc, hidden_states, Wq_bytes, Wq_scale, Wk
                 in_=il[:],
             )
 
-        widen(0, 0, (1,), "v")
-        widen(0, 0, (0,), "s")
+        widen(0, 0, (1, 3), "v")
+        widen(0, 0, (0, 2), "s")
+        widen(0, 1, (1, 3), "v")
+        widen(0, 1, (0, 2), "s")
         make_tables()
-        widen(0, 0, (2, 3), "s")
-        widen(0, 1)
-        il_k(0)
-        il_k(1)
-        quant_k(0)
         il_q(0, 0, ROT, "v")
         il_q(0, 0, PLAIN, "v")
-        il_k(2)
-        il_k(3)
+        il_q(0, 1, ROT, "v")
+        il_q(0, 1, PLAIN, "v")
         quant_q(0, 0)
+        widen(0, 2)
+        il_k(0)
+        quant_q(0, 1)
+        il_k(1)
+        turn_x(0)
+        quant_x(0)
+        il_q(0, 2, ROT, "v")
+        il_q(0, 2, PLAIN, "v")
+        quant_k(0)
+        widen(0, 3)
+        quant_q(0, 2)
+        il_k(2)
+        il_k(3, eng="s")
         for g in range(G):
             load_v(g)
         for g in (2, 3):
             load_q(1, g, 0, 2)
             load_q(1, g, 2, 2)
-        widen(0, 2)
-        il_q(0, 1, ROT, "v")
-        il_q(0, 1, PLAIN, "v")
-        quant_k(1)
-        turn_x(0)
-        quant_q(0, 1)
-        widen(0, 3, (0,), "v")
-        widen(0, 3, (1, 2, 3), "s")
-        il_q(0, 2, ROT, "v")
-        il_q(0, 2, PLAIN, "v")
-        quant_x(0)
         turn_x(1)
-        quant_q(0, 2)
+        quant_k(1)
         quant_x(1)
         banks_v0 = fill_v(0)
         widen(1, 0)

@@ -90,12 +90,12 @@ def tile_diffucoderattention_pa_kernel(tc, hidden_states, Wq_bytes, Wq_scale, Wk
         load_q(0, 0, 2, 2)
         load_q(0, 1, 0, 2)
         load_q(0, 1, 2, 2)
-        load_k(0)
         load_q(0, 2, 0, 2)
         load_q(0, 2, 2, 2)
-        load_k(1)
         load_x(0)
         load_x(1)
+        load_k(0)
+        load_k(1)
         load_q(0, 3, 0, 2)
         load_q(0, 3, 2, 2)
         load_k(2)
@@ -233,6 +233,29 @@ def tile_diffucoderattention_pa_kernel(tc, hidden_states, Wq_bytes, Wq_scale, Wk
                     ilk_of[gp][:, lo:hi].rearrange("p (c i t) -> p c t i", i=RUN, t=PACK),
                     tl[:].rearrange("p t (c i) -> p c t i", i=RUN),
                 )
+
+        def fill_kg(g, side):
+            banks = []
+            for b in range(2):
+                bank = psum.tile([P, 1024], BF16, name="rt", tag=side)
+                for k in range(2):
+                    nc.tensor.matmul(
+                        out=bank[:].rearrange("p (c t) -> p t c", t=PACK)[:, 2 * k : 2 * k + 2, :],
+                        lhsT=ident_b[:],
+                        rhs=wk_raw[g][0][2][:, 2 * k : 2 * k + 2, b * 256 : (b + 1) * 256],
+                        start=True,
+                        stop=True,
+                    )
+                banks.append(bank)
+            return banks
+
+        def empty_kg(g, banks):
+            gp = g // 2
+            if gp not in ilk_of:
+                ilk_of[gp] = ilp.tile([P, 4096], BF16, name="il", tag="il", align_bytes=64)
+            for b in range(2):
+                lo = (g % 2) * 2048 + b * 1024
+                copy_on("s", ilk_of[gp][:, lo : lo + 1024].bitcast(F32), banks[b][:].bitcast(F32))
 
         def quant_k(gp):
             nc.vector.quantize_mx(
@@ -419,22 +442,26 @@ def tile_diffucoderattention_pa_kernel(tc, hidden_states, Wq_bytes, Wq_scale, Wk
         make_tables()
         il_q(0, 0, ROT, "v")
         il_q(0, 0, PLAIN, "v")
+        widen(0, 2, (1, 3), "v")
+        widen(0, 2, (0, 2), "s")
         il_q(0, 1, ROT, "v")
         il_q(0, 1, PLAIN, "v")
         quant_q(0, 0)
-        widen(0, 2)
-        il_k(0)
-        quant_q(0, 1)
-        il_k(1)
         turn_x(0)
+        banks_k1 = fill_kg(1, "A")
+        il_k(0)
+        empty_kg(1, banks_k1)
+        quant_q(0, 1)
         quant_x(0)
+        banks_k2 = fill_kg(2, "B")
         il_q(0, 2, ROT, "v")
         il_q(0, 2, PLAIN, "v")
         quant_k(0)
         widen(0, 3)
         quant_q(0, 2)
-        il_k(2)
-        il_k(3, eng="s")
+        banks_k3 = fill_kg(3, "A")
+        empty_kg(2, banks_k2)
+        empty_kg(3, banks_k3)
         for g in range(G):
             load_v(g)
         for g in (2, 3):
@@ -442,6 +469,7 @@ def tile_diffucoderattention_pa_kernel(tc, hidden_states, Wq_bytes, Wq_scale, Wk
             load_q(1, g, 2, 2)
         turn_x(1)
         quant_k(1)
+        il_q(0, 3, ROT, "v")
         quant_x(1)
         banks_v0 = fill_v(0)
         widen(1, 0)
@@ -449,7 +477,6 @@ def tile_diffucoderattention_pa_kernel(tc, hidden_states, Wq_bytes, Wq_scale, Wk
         passes(k_acc, kc[:, :, :], ks[:, :, :])
         il_v0 = empty_v(banks_v0)
         banks_v1 = fill_v(1)
-        il_q(0, 3, ROT, "v")
         il_q(0, 3, PLAIN, "v")
         widen(1, 1)
 

@@ -450,6 +450,7 @@ def tile_diffucoderattention_pa_kernel(tc, hidden_states, Wq_bytes, Wq_scale, Wk
         turn_x(0)
         banks_k1 = fill_kg(1, "A")
         il_k(0)
+        widen(0, 3, (0, 1))
         empty_kg(1, banks_k1)
         quant_q(0, 1)
         quant_x(0)
@@ -457,7 +458,7 @@ def tile_diffucoderattention_pa_kernel(tc, hidden_states, Wq_bytes, Wq_scale, Wk
         il_q(0, 2, ROT, "v")
         il_q(0, 2, PLAIN, "v")
         quant_k(0)
-        widen(0, 3)
+        widen(0, 3, (2, 3))
         quant_q(0, 2)
         banks_k3 = fill_kg(3, "A")
         empty_kg(2, banks_k2)

@@ -102,9 +102,6 @@ def tile_diffucoderattention_pa_kernel(tc, hidden_states, Wq_bytes, Wq_scale, Wk
         load_k(3)
         load_x(2)
         load_x(3)
-        for j, g in ((1, 0), (1, 1)):
-            load_q(j, g, 0, 2)
-            load_q(j, g, 2, 2)
 
         warm = const.tile([P, 2 + PAD_COLUMNS], F32, name="warm")
         nc.vector.memset(warm[:, 0:2], 0.0)
@@ -450,6 +447,11 @@ def tile_diffucoderattention_pa_kernel(tc, hidden_states, Wq_bytes, Wq_scale, Wk
         turn_x(0)
         banks_k1 = fill_kg(1, "A")
         il_k(0)
+        load_v(0)
+        load_v(1)
+        for j, g in ((1, 0), (1, 1)):
+            load_q(j, g, 0, 2)
+            load_q(j, g, 2, 2)
         widen(0, 3, (0, 1))
         empty_kg(1, banks_k1)
         quant_q(0, 1)
@@ -463,8 +465,8 @@ def tile_diffucoderattention_pa_kernel(tc, hidden_states, Wq_bytes, Wq_scale, Wk
         banks_k3 = fill_kg(3, "A")
         empty_kg(2, banks_k2)
         empty_kg(3, banks_k3)
-        for g in range(G):
-            load_v(g)
+        load_v(2)
+        load_v(3)
         for g in (2, 3):
             load_q(1, g, 0, 2)
             load_q(1, g, 2, 2)

@@ -177,14 +177,14 @@ def tile_diffucoderattention_pa_kernel(tc, hidden_states, Wq_bytes, Wq_scale, Wk
 
         il_of = {}
 
-        def il_q(j, g, half, eng):
+        def il_q(j, g, half, eng, h0=0, h1=8):
             if (j, g) not in il_of:
                 il_of[(j, g)] = ilp.tile([P, 4096], BF16, name="il", tag="il", align_bytes=64)
             dst = il_of[(j, g)][:, half * 2048 : (half + 1) * 2048]
             copy_on(
                 eng,
-                dst.rearrange("p (h c i t) -> p h c t i", h=8, i=RUN, t=PACK),
-                wide[(j, g)][:].rearrange("p t (h c i) -> p h c t i", h=8, i=RUN)[:, :, half * (64 // RUN) : (half + 1) * (64 // RUN), :, :],
+                dst.rearrange("p (h c i t) -> p h c t i", h=8, i=RUN, t=PACK)[:, h0:h1, :, :, :],
+                wide[(j, g)][:].rearrange("p t (h c i) -> p h c t i", h=8, i=RUN)[:, h0:h1, half * (64 // RUN) : (half + 1) * (64 // RUN), :, :],
             )
 
         def fill_q(j, g, half, side="B"):
@@ -472,16 +472,25 @@ def tile_diffucoderattention_pa_kernel(tc, hidden_states, Wq_bytes, Wq_scale, Wk
             load_q(1, g, 2, 2)
         turn_x(1)
         quant_k(1)
+        banks_v0 = fill_vg(0, "B")
+        k_acc = banks_of("A")
+        for tt in range(2):
+            for g in range(G):
+                one_pass(k_acc[tt][:], tt, g, kc[:, :, :], ks[:, :, :])
         il_q(0, 3, ROT, "v")
         quant_x(1)
-        banks_v0 = fill_v(0)
         widen(1, 0)
-        k_acc = banks_of("A")
-        passes(k_acc, kc[:, :, :], ks[:, :, :])
-        il_v0 = empty_v(banks_v0)
-        banks_v1 = fill_v(1)
+        for tt in range(2, TT):
+            for g in range(G):
+                one_pass(k_acc[tt][:], tt, g, kc[:, :, :], ks[:, :, :])
+        empty_vg(0, banks_v0)
+        banks_v0b = fill_vg(1, "B")
         il_q(0, 3, PLAIN, "v")
-        widen(1, 1)
+        widen(1, 1, (0, 1))
+        empty_vg(1, banks_v0b)
+        il_v0 = ilv_of[0]
+        banks_v1 = fill_v(1)
+        widen(1, 1, (2, 3))
 
         y_k = {}
         for tt in range(TT):
@@ -531,11 +540,12 @@ def tile_diffucoderattention_pa_kernel(tc, hidden_states, Wq_bytes, Wq_scale, Wk
         il_q(1, 2, ROT, "v")
         il_q(1, 2, PLAIN, "s")
         il_q(1, 3, ROT, "v")
-        il_q(1, 3, PLAIN, "s")
+        il_q(1, 3, PLAIN, "s", 0, 4)
         quant_q(1, 2, (ROT,))
         passes(rot_acc, *q_half(1, ROT), gs=(2,))
         quant_q(1, 3, (ROT,))
         passes(rot_acc, *q_half(1, ROT), gs=(3,))
+        il_q(1, 3, PLAIN, "v", 4, 8)
         quant_q(1, 2, (PLAIN,))
         quant_q(1, 3, (PLAIN,))
         plain_acc = {}

@@ -211,6 +211,32 @@ def tile_diffucoderattention_pa_kernel(tc, hidden_states, Wq_bytes, Wq_scale, Wk
                 lo = half * 2048 + b * 1024
                 copy_on(eng, il_of[(j, g)][:, lo : lo + 1024].bitcast(F32), banks[b][:].bitcast(F32))
 
+        def fill_qc(j, g, first, sides):
+            banks = []
+            for side in sides:
+                bank = psum.tile([P, 1024], BF16, name="rq", tag=side)
+                banks.append(bank)
+            for k in range(2):
+                for n in range(len(sides)):
+                    b = first + n
+                    nc.tensor.matmul(
+                        out=banks[n][:].rearrange("p (c t) -> p t c", t=PACK)[:, 2 * k : 2 * k + 2, :],
+                        lhsT=ident_b[:],
+                        rhs=wide[(j, g)][:, 2 * k : 2 * k + 2, b * 256 : (b + 1) * 256],
+                        start=True,
+                        stop=True,
+                    )
+            return banks
+
+        def empty_qc(j, g, b, bank, eng="s"):
+            if (j, g) not in il_of:
+                il_of[(j, g)] = ilp.tile([P, 4096], BF16, name="il", tag="il", align_bytes=64)
+            copy_on(
+                eng,
+                il_of[(j, g)][:].bitcast(F32).rearrange("p (half h x) -> p h half x", half=2, h=8)[:, 2 * b : 2 * b + 2, :, :],
+                bank[:].bitcast(F32).rearrange("p (h half x) -> p h half x", h=2, half=2),
+            )
+
         def quant_q(j, g, halves=(ROT, PLAIN)):
             lo = halves[0] * 512
             hi = (halves[-1] + 1) * 512
@@ -436,11 +462,14 @@ def tile_diffucoderattention_pa_kernel(tc, hidden_states, Wq_bytes, Wq_scale, Wk
         widen(0, 0, (0, 2), "s")
         widen(0, 1, (1, 3), "v")
         widen(0, 1, (0, 2), "s")
+        banks_q00 = fill_qc(0, 0, 0, ("A", "B"))
         make_tables()
-        il_q(0, 0, ROT, "v")
-        il_q(0, 0, PLAIN, "v")
-        widen(0, 2, (1, 3), "v")
-        widen(0, 2, (0, 2), "s")
+        il_q(0, 0, ROT, "v", 4, 8)
+        il_q(0, 0, PLAIN, "v", 4, 8)
+        empty_qc(0, 0, 0, banks_q00[0])
+        empty_qc(0, 0, 1, banks_q00[1])
+        widen(0, 2, (0, 1, 3), "v")
+        widen(0, 2, (2,), "s")
         il_q(0, 1, ROT, "v")
         il_q(0, 1, PLAIN, "v")
         quant_q(0, 0)

@@ -569,12 +569,12 @@ def tile_diffucoderattention_pa_kernel(tc, hidden_states, Wq_bytes, Wq_scale, Wk
         il_q(1, 2, ROT, "v")
         il_q(1, 2, PLAIN, "s")
         il_q(1, 3, ROT, "v")
-        il_q(1, 3, PLAIN, "s", 0, 4)
+        il_q(1, 3, PLAIN, "s", 0, 6)
         quant_q(1, 2, (ROT,))
         passes(rot_acc, *q_half(1, ROT), gs=(2,))
         quant_q(1, 3, (ROT,))
         passes(rot_acc, *q_half(1, ROT), gs=(3,))
-        il_q(1, 3, PLAIN, "v", 4, 8)
+        il_q(1, 3, PLAIN, "v", 6, 8)
         quant_q(1, 2, (PLAIN,))
         quant_q(1, 3, (PLAIN,))
         plain_acc = {}

@@ -327,6 +327,13 @@ def tile_diffucoderattention_pa_kernel(tc, hidden_states, Wq_bytes, Wq_scale, Wk
                 lo = (g % 2) * 2048 + b * 1024
                 copy_on("s", ilv_of[g // 2][:, lo : lo + 1024].bitcast(F32), banks[b][:].bitcast(F32))
 
+        def il_v3(eng, c0, c1):
+            copy_on(
+                eng,
+                ilv_of[1][:, 2048 + PACK * c0 : 2048 + PACK * c1].rearrange("p (c i t) -> p c t i", i=RUN, t=PACK),
+                wv_raw[3][:, :, c0:c1].rearrange("p t (c i) -> p c t i", i=RUN),
+            )
+
         def empty_v(banks):
             il = ilp.tile([P, 4096], BF16, name="ilt", tag="ilt", bufs=2, align_bytes=64)
             for b in range(4):
@@ -518,7 +525,7 @@ def tile_diffucoderattention_pa_kernel(tc, hidden_states, Wq_bytes, Wq_scale, Wk
         widen(1, 1, (0, 1))
         empty_vg(1, banks_v0b)
         il_v0 = ilv_of[0]
-        banks_v1 = fill_v(1)
+        banks_v2 = fill_vg(2, "B")
         widen(1, 1, (2, 3))
 
         y_k = {}
@@ -529,7 +536,9 @@ def tile_diffucoderattention_pa_kernel(tc, hidden_states, Wq_bytes, Wq_scale, Wk
             copy_on("v" if tt < 2 else "s", heads_of(y_k[tt][:], 128)[:, :, 64:128], heads_of(k_acc[tt][:], 128)[:, :, 64:128])
             nc.sync.dma_start(out=k_out[tt * P : (tt + 1) * P, :], in_=y_k[tt][:])
 
-        il_v1 = empty_v(banks_v1)
+        empty_vg(2, banks_v2)
+        il_v1 = ilv_of[1]
+        il_v3("s", 256, 512)
         quant_q(0, 3)
         il_q(1, 0, ROT, "v")
         il_q(1, 0, PLAIN, "v")
@@ -541,6 +550,7 @@ def tile_diffucoderattention_pa_kernel(tc, hidden_states, Wq_bytes, Wq_scale, Wk
         quant_v(0, il_v0)
         quant_q(1, 0)
         widen(1, 3)
+        il_v3("v", 0, 256)
         il_q(1, 1, ROT, "v")
         il_q(1, 1, PLAIN, "v")
         quant_v(1, il_v1)

@@ -526,6 +526,15 @@ def tile_diffucoderattention_pa_kernel(tc, hidden_states, Wq_bytes, Wq_scale, Wk
         empty_vg(1, banks_v0b)
         il_v0 = ilv_of[0]
         banks_v2 = fill_vg(2, "B")
+        bank_v3 = psum.tile([P, 1024], BF16, name="rt", tag="B")
+        for k in range(2):
+            nc.tensor.matmul(
+                out=bank_v3[:].rearrange("p (c t) -> p t c", t=PACK)[:, 2 * k : 2 * k + 2, :],
+                lhsT=ident_b[:],
+                rhs=wv_raw[3][:, 2 * k : 2 * k + 2, 256:512],
+                start=True,
+                stop=True,
+            )
         widen(1, 1, (2, 3))
 
         y_k = {}
@@ -538,7 +547,7 @@ def tile_diffucoderattention_pa_kernel(tc, hidden_states, Wq_bytes, Wq_scale, Wk
 
         empty_vg(2, banks_v2)
         il_v1 = ilv_of[1]
-        il_v3("s", 256, 512)
+        copy_on("s", ilv_of[1][:, 3072:4096].bitcast(F32), bank_v3[:].bitcast(F32))
         quant_q(0, 3)
         il_q(1, 0, ROT, "v")
         il_q(1, 0, PLAIN, "v")

@@ -328,6 +328,8 @@ def tile_diffucoderattention_pa_kernel(tc, hidden_states, Wq_bytes, Wq_scale, Wk
                 copy_on("s", ilv_of[g // 2][:, lo : lo + 1024].bitcast(F32), banks[b][:].bitcast(F32))
 
         def il_v3(eng, c0, c1):
+            if 1 not in ilv_of:
+                ilv_of[1] = ilp.tile([P, 4096], BF16, name="ilt", tag="ilt", bufs=2, align_bytes=64)
             copy_on(
                 eng,
                 ilv_of[1][:, 2048 + PACK * c0 : 2048 + PACK * c1].rearrange("p (c i t) -> p c t i", i=RUN, t=PACK),
@@ -536,6 +538,7 @@ def tile_diffucoderattention_pa_kernel(tc, hidden_states, Wq_bytes, Wq_scale, Wk
                 stop=True,
             )
         widen(1, 1, (2, 3))
+        il_v3("v", 0, 256)
 
         y_k = {}
         for tt in range(TT):
@@ -559,7 +562,6 @@ def tile_diffucoderattention_pa_kernel(tc, hidden_states, Wq_bytes, Wq_scale, Wk
         quant_v(0, il_v0)
         quant_q(1, 0)
         widen(1, 3)
-        il_v3("v", 0, 256)
         il_q(1, 1, ROT, "v")
         il_q(1, 1, PLAIN, "v")
         quant_v(1, il_v1)

import math
from contextlib import ExitStack

import concourse.mybir as mybir

FLOPS = 2 * 512 * 2048 * 3072

F32 = mybir.dt.float32
BF16 = mybir.dt.bfloat16
U32 = mybir.dt.uint32
U8 = mybir.dt.uint8
I32 = mybir.dt.int32
FP8 = mybir.dt.float8_e4m3fn
FP8X4 = mybir.dt.float8_e4m3fn_x4
ALU = mybir.AluOpType
ACT = mybir.ActivationFunctionType

P = 128
PACK = 4
TT = 4
G = 4
PAIRS = 32
FREQ_STEP = 10000.0 ** (-1.0 / 32.0)
RUN = 8
PAD_COLUMNS = 392
ROT = 0
PLAIN = 1


def tile_diffucoderattention_pa_kernel(tc, hidden_states, Wq_bytes, Wq_scale, Wk, Wv, out_0, out_1, out_2):
    nc = tc.nc
    x_rows = hidden_states.rearrange("o s k -> (o s) k")
    q_out = out_0.rearrange("o s h d -> (o s) (h d)")
    k_out = out_1.rearrange("o s h d -> (o s) (h d)")
    v_out = out_2.rearrange("o s h d -> (o s) (h d)")
    wq_view = Wq_bytes.rearrange("(g p t) n -> g p t n", p=P, t=PACK)
    wk_view = Wk.rearrange("(g p t) n -> g p t n", p=P, t=PACK)
    wv_view = Wv.rearrange("(g p t) n -> g p t n", p=P, t=PACK)

    with ExitStack() as ctx:
        const = ctx.enter_context(tc.tile_pool(name="const", bufs=1))
        raw = ctx.enter_context(tc.tile_pool(name="raw", bufs=1))
        keep = ctx.enter_context(tc.tile_pool(name="keep", bufs=1))
        xy = ctx.enter_context(tc.tile_pool(name="xy", bufs=6))
        widep = ctx.enter_context(tc.tile_pool(name="widep", bufs=4))
        ilp = ctx.enter_context(tc.tile_pool(name="ilp", bufs=3))
        zp = ctx.enter_context(tc.tile_pool(name="zp", bufs=3))
        psum = ctx.enter_context(tc.psum_pool(name="psum", bufs=4))

        ctx.enter_context(tc.manual_schedule())

        scl = const.tile([P, G * PACK], F32, name="scl")
        plane = {}
        wk_raw = {}
        wv_raw = {}
        x_sb = {}

        def load_scl():
            nc.scalar.dma_start(
                out=scl[:].rearrange("p (g t) -> p g t", t=PACK),
                in_=Wq_scale.rearrange("(g p t) o -> p g (t o)", p=P, t=PACK),
            )

        def load_q(j, g, t0, nt):
            tl = raw.tile([P, nt, 1024], U8, name="wq_bytes_%d_%d_%d" % (j, g, t0))
            nc.sync.dma_start(out=tl[:], in_=wq_view[g][:, t0 : t0 + nt, j * 1024 : (j + 1) * 1024])
            for t in range(nt):
                plane[(j, g, t0 + t)] = tl[:, t, :]

        def load_k(g, c0=0, c1=512):
            if c1 - c0 == 512:
                tl = raw.tile([P, PACK, 512], BF16, name="wk_raw", tag="wkv", bufs=4)
            else:
                tl = raw.tile([P, PACK, c1 - c0], BF16, name="wk_part_%d_%d" % (g, c0))
            nc.sync.dma_start(out=tl[:], in_=wk_view[g][:, :, c0:c1])
            wk_raw.setdefault(g, []).append((c0, c1, tl))

        def load_v(g):
            tl = raw.tile([P, PACK, 512], BF16, name="wv_raw", tag="wkv", bufs=4)
            nc.sync.dma_start(out=tl[:], in_=wv_view[g])
            wv_raw[g] = tl

        def load_x(tt):
            tl = xy.tile([P, 2048], BF16, name="x_sb_%d" % tt, tag="xy")
            nc.sync.dma_start(out=tl[:], in_=x_rows[tt * P : (tt + 1) * P, :])
            x_sb[tt] = tl

        load_scl()
        load_q(0, 0, 0, 2)
        load_q(0, 0, 2, 2)
        load_q(0, 1, 0, 2)
        load_q(0, 1, 2, 2)
        load_q(0, 2, 0, 2)
        load_q(0, 2, 2, 2)
        load_x(0)
        load_x(1)
        load_k(0)
        load_k(1)
        load_q(0, 3, 0, 2)
        load_q(0, 3, 2, 2)
        load_k(2)
        load_k(3)
        load_x(2)
        load_x(3)

        warm = const.tile([P, 2 + PAD_COLUMNS], F32, name="warm")
        nc.vector.memset(warm[:, 0:2], 0.0)
        nc.scalar.activation(out=warm[:, 1:2], in_=warm[:, 0:1], func=ACT.Sin)

        turns = const.tile([P, TT, PAIRS], F32, name="turns")
        nc.gpsimd.iota(
            turns[:].rearrange("p t i -> p (t i)"), pattern=[[P, TT], [0, PAIRS]], base=0, channel_multiplier=1,
            allow_small_or_imprecise_dtypes=True,
        )
        diag = const.tile([P, P], F32, name="diag")
        nc.gpsimd.iota(diag[:], pattern=[[-1, P]], base=0, channel_multiplier=1, allow_small_or_imprecise_dtypes=True)

        by_ab = turns[:].rearrange("p t (a b) -> p t a b", b=8)
        for a in range(4):
            nc.vector.tensor_scalar(
                out=by_ab[:, :, a, :], in0=by_ab[:, :, a, :], scalar1=FREQ_STEP ** (8 * a) / (2.0 * math.pi), scalar2=None, op0=ALU.mult
            )
        for b in range(1, 8):
            nc.vector.tensor_scalar(out=by_ab[:, :, :, b], in0=by_ab[:, :, :, b], scalar1=FREQ_STEP**b, scalar2=None, op0=ALU.mult)
        ident = const.tile([P, P], F32, name="ident")
        nc.vector.tensor_scalar(out=ident[:], in0=diag[:], scalar1=0.0, scalar2=None, op0=ALU.is_equal)
        turns_flat = turns[:].rearrange("p t i -> p (t i)")
        whole = const.tile([P, TT * PAIRS], I32, name="whole")
        nc.vector.tensor_copy(out=whole[:], in_=turns_flat)
        ident_b = const.tile([P, P], BF16, name="ident_b")
        nc.vector.tensor_scalar(out=ident_b[:], in0=diag[:], scalar1=0.0, scalar2=None, op0=ALU.is_equal)
        frac = const.tile([P, TT * PAIRS], F32, name="frac")
        nc.vector.tensor_tensor(out=frac[:], in0=turns_flat, in1=whole[:], op=ALU.subtract)
        afrac = const.tile([P, TT * PAIRS], F32, name="afrac")
        nc.vector.scalar_tensor_tensor(out=afrac[:], in0=frac[:], scalar=-1.0, in1=frac[:], op0=ALU.mult, op1=ALU.max)
        frac3 = frac[:].rearrange("p (t i) -> p t i", i=PAIRS)
        afrac3 = afrac[:].rearrange("p (t i) -> p t i", i=PAIRS)
        tab = const.tile([P, 3, TT, PAIRS], F32, name="tab")

        def make_tables():
            nc.scalar.activation(out=tab[:, 0, :, :], in_=frac3, func=ACT.Sin, scale=-2.0 * math.pi)
            nc.scalar.activation(out=tab[:, 2, :, :], in_=frac3, func=ACT.Sin, scale=2.0 * math.pi)
            nc.scalar.activation(out=tab[:, 1, :, :], in_=afrac3, func=ACT.Sin, scale=-2.0 * math.pi, bias=math.pi / 2.0)

        xc = {}
        xs = {}
        for tp in range(2):
            xc[tp] = keep.tile([P, 2 * G * P], U32, name="xc_%d" % tp, align_bytes=256)
            xs[tp] = keep.tile([P, 2 * G * P], U8, name="xs_%d" % tp, align_bytes=256)
        qc = {}
        qs = {}
        for j in range(2):
            qc[j] = keep.tile([P, G, 1024], U32, name="qc_%d" % j, align_bytes=256)
            qs[j] = keep.tile([P, G, 1024], U8, name="qs_%d" % j, align_bytes=256)
        kc = keep.tile([P, G, 512], U32, name="kc", tag="kvc", align_bytes=256)
        ks = keep.tile([P, G, 512], U8, name="ks", tag="kvs", align_bytes=256)

        def copy_on(eng, out, in_):
            if eng == "v":
                nc.vector.tensor_copy(out=out, in_=in_)
            else:
                nc.scalar.copy(out=out, in_=in_)

        wide = {}

        def widen(j, g, planes=(0, 1, 2, 3), eng="s"):
            if (j, g) not in wide:
                wide[(j, g)] = widep.tile([P, PACK, 1024], BF16, name="wide", tag="wide")
            tl = wide[(j, g)]
            for t in planes:
                src = plane[(j, g, t)].bitcast(FP8)
                col = scl[:, PACK * g + t : PACK * g + t + 1]
                if eng == "v":
                    nc.vector.tensor_scalar(out=tl[:, t, :], in0=src, scalar1=col, scalar2=None, op0=ALU.mult)
                else:
                    nc.scalar.activation(out=tl[:, t, :], in_=src, func=ACT.Copy, scale=col)

        il_of = {}

        def il_q(j, g, half, eng, h0=0, h1=8):
            if (j, g) not in il_of:
                il_of[(j, g)] = ilp.tile([P, 4096], BF16, name="il", tag="il", align_bytes=64)
            dst = il_of[(j, g)][:, half * 2048 : (half + 1) * 2048]
            copy_on(
                eng,
                dst.rearrange("p (h c i t) -> p h c t i", h=8, i=RUN, t=PACK)[:, h0:h1, :, :, :],
                wide[(j, g)][:].rearrange("p t (h c i) -> p h c t i", h=8, i=RUN)[:, h0:h1, half * (64 // RUN) : (half + 1) * (64 // RUN), :, :],
            )

        def fill_q(j, g, half, side="B"):
            banks = []
            for b in range(2):
                bank = psum.tile([P, 1024], BF16, name="rq", tag=side)
                for k in range(2):
                    nc.tensor.matmul(
                        out=bank[:].rearrange("p (h f t) -> p t h f", h=4, t=PACK)[:, 2 * k : 2 * k + 2, :, :],
                        lhsT=ident_b[:],
                        rhs=wide[(j, g)][:, 2 * k : 2 * k + 2, :].rearrange("p t (h f) -> p t h f", f=128)[
                            :, :, 4 * b : 4 * b + 4, half * 64 : (half + 1) * 64
                        ],
                        start=True,
                        stop=True,
                    )
                banks.append(bank)
            return banks

        def empty_q(j, g, half, banks, eng="s"):
            if (j, g) not in il_of:
                il_of[(j, g)] = ilp.tile([P, 4096], BF16, name="il", tag="il", align_bytes=64)
            for b in range(2):
                lo = half * 2048 + b * 1024
                copy_on(eng, il_of[(j, g)][:, lo : lo + 1024].bitcast(F32), banks[b][:].bitcast(F32))

        def fill_qc(j, g, first, sides):
            banks = []
            for side in sides:
                bank = psum.tile([P, 1024], BF16, name="rq", tag=side)
                banks.append(bank)
            for k in range(2):
                for n in range(len(sides)):
                    b = first + n
                    nc.tensor.matmul(
                        out=banks[n][:].rearrange("p (c t) -> p t c", t=PACK)[:, 2 * k : 2 * k + 2, :],
                        lhsT=ident_b[:],
                        rhs=wide[(j, g)][:, 2 * k : 2 * k + 2, b * 256 : (b + 1) * 256],
                        start=True,
                        stop=True,
                    )
            return banks

        def empty_qc(j, g, b, bank, eng="s"):
            if (j, g) not in il_of:
                il_of[(j, g)] = ilp.tile([P, 4096], BF16, name="il", tag="il", align_bytes=64)
            copy_on(
                eng,
                il_of[(j, g)][:].bitcast(F32).rearrange("p (half h x) -> p h half x", half=2, h=8)[:, 2 * b : 2 * b + 2, :, :],
                bank[:].bitcast(F32).rearrange("p (h half x) -> p h half x", h=2, half=2),
            )

        def quant_q(j, g, halves=(ROT, PLAIN)):
            lo = halves[0] * 512
            hi = (halves[-1] + 1) * 512
            nc.vector.quantize_mx(out=qc[j][:, g, lo:hi].bitcast(FP8X4), scales=qs[j][:, g, lo:hi], in_=il_of[(j, g)][:, 4 * lo : 4 * hi])

        ilk_of = {}

        def il_k(g, first=0, last=None, eng="v"):
            gp = g // 2
            if gp not in ilk_of:
                ilk_of[gp] = ilp.tile([P, 4096], BF16, name="il", tag="il", align_bytes=64)
            for c0, c1, tl in wk_raw[g][first:last]:
                lo = (g % 2) * 2048 + PACK * c0
                hi = (g % 2) * 2048 + PACK * c1
                copy_on(
                    eng,
                    ilk_of[gp][:, lo:hi].rearrange("p (c i t) -> p c t i", i=RUN, t=PACK),
                    tl[:].rearrange("p t (c i) -> p c t i", i=RUN),
                )

        def fill_kg(g, side):
            banks = []
            for b in range(2):
                bank = psum.tile([P, 1024], BF16, name="rt", tag=side)
                for k in range(2):
                    nc.tensor.matmul(
                        out=bank[:].rearrange("p (c t) -> p t c", t=PACK)[:, 2 * k : 2 * k + 2, :],
                        lhsT=ident_b[:],
                        rhs=wk_raw[g][0][2][:, 2 * k : 2 * k + 2, b * 256 : (b + 1) * 256],
                        start=True,
                        stop=True,
                    )
                banks.append(bank)
            return banks

        def empty_kg(g, banks):
            gp = g // 2
            if gp not in ilk_of:
                ilk_of[gp] = ilp.tile([P, 4096], BF16, name="il", tag="il", align_bytes=64)
            for b in range(2):
                lo = (g % 2) * 2048 + b * 1024
                copy_on("s", ilk_of[gp][:, lo : lo + 1024].bitcast(F32), banks[b][:].bitcast(F32))

        def quant_k(gp):
            nc.vector.quantize_mx(
                out=kc[:, 2 * gp : 2 * gp + 2, :].rearrange("p g n -> p (g n)").bitcast(FP8X4),
                scales=ks[:, 2 * gp : 2 * gp + 2, :].rearrange("p g n -> p (g n)"),
                in_=ilk_of[gp][:],
            )

        def fill_v(gp):
            banks = []
            for gl in range(2):
                for b in range(2):
                    bank = psum.tile([P, 1024], BF16, name="rt", tag="B")
                    for k in range(2):
                        nc.tensor.matmul(
                            out=bank[:].rearrange("p (c t) -> p t c", t=PACK)[:, 2 * k : 2 * k + 2, :],
                            lhsT=ident_b[:],
                            rhs=wv_raw[2 * gp + gl][:, 2 * k : 2 * k + 2, b * 256 : (b + 1) * 256],
                            start=True,
                            stop=True,
                        )
                    banks.append(bank)
            return banks

        def fill_vg(g, side="B"):
            banks = []
            for b in range(2):
                bank = psum.tile([P, 1024], BF16, name="rt", tag=side)
                for k in range(2):
                    nc.tensor.matmul(
                        out=bank[:].rearrange("p (c t) -> p t c", t=PACK)[:, 2 * k : 2 * k + 2, :],
                        lhsT=ident_b[:],
                        rhs=wv_raw[g][:, 2 * k : 2 * k + 2, b * 256 : (b + 1) * 256],
                        start=True,
                        stop=True,
                    )
                banks.append(bank)
            return banks

        ilv_of = {}

        def empty_vg(g, banks):
            if g // 2 not in ilv_of:
                ilv_of[g // 2] = ilp.tile([P, 4096], BF16, name="ilt", tag="ilt", bufs=2, align_bytes=64)
            for b in range(2):
                lo = (g % 2) * 2048 + b * 1024
                copy_on("s", ilv_of[g // 2][:, lo : lo + 1024].bitcast(F32), banks[b][:].bitcast(F32))

        def il_v3(eng, c0, c1):
            if 1 not in ilv_of:
                ilv_of[1] = ilp.tile([P, 4096], BF16, name="ilt", tag="ilt", bufs=2, align_bytes=64)
            copy_on(
                eng,
                ilv_of[1][:, 2048 + PACK * c0 : 2048 + PACK * c1].rearrange("p (c i t) -> p c t i", i=RUN, t=PACK),
                wv_raw[3][:, :, c0:c1].rearrange("p t (c i) -> p c t i", i=RUN),
            )

        def empty_v(banks):
            il = ilp.tile([P, 4096], BF16, name="ilt", tag="ilt", bufs=2, align_bytes=64)
            for b in range(4):
                copy_on("s", il[:, b * 1024 : (b + 1) * 1024].bitcast(F32), banks[b][:].bitcast(F32))
            return il

        def one_pass(acc, tt, g, codes, scales):
            lo = (tt % 2) * 512 + g * P
            nc.tensor.matmul_mx(
                out=acc,
                lhsT=xc[tt // 2][:, lo : lo + P].bitcast(FP8X4),
                lhsT_scale=xs[tt // 2][:, lo : lo + P],
                rhs=codes[:, g, :].bitcast(FP8X4),
                rhs_scale=scales[:, g, :],
                start=(g == 0),
                stop=(g == G - 1),
            )

        def banks_of(side):
            accs = []
            for tt in range(TT):
                acc = psum.tile([P, 512], F32, name="acc", tag=side)
                accs.append(acc)
            return accs

        def passes(accs, codes, scales, gs=(0, 1, 2, 3), by_bank=True):
            if by_bank:
                for tt in range(TT):
                    for g in gs:
                        one_pass(accs[tt][:], tt, g, codes, scales)
            else:
                for g in gs:
                    for tt in range(TT):
                        one_pass(accs[tt][:], tt, g, codes, scales)

        def q_half(j, half):
            return qc[j][:, :, half * 512 : (half + 1) * 512], qs[j][:, :, half * 512 : (half + 1) * 512]

        def heads_of(ap, width):
            return ap.rearrange("p (h f) -> p h f", f=width)

        def rope_products(tt, rot, both=True):
            heads = rot.shape[1]
            n = heads * 64
            z = zp.tile([P, 2, 512], F32, name="z", tag="z")
            shape = [P, heads, PAIRS, 2]
            for r in range(2):
                nc.vector.tensor_tensor(
                    out=z[:, r, 0:n].rearrange("p (h i e) -> p h i e", h=heads, e=2),
                    in0=rot.rearrange("p h (i e) -> p h i e", e=2)[:, :, :, r : r + 1].to_broadcast(shape),
                    in1=tab[:, 1 - r : 3 - r, tt, :].rearrange("p e i -> p i e").unsqueeze(1).to_broadcast(shape),
                    op=ALU.mult,
                )
            return z[:, :, 0:n]

        def rope_sum(z, y_rot, add_eng):
            add_eng.tensor_tensor(out=y_rot, in0=heads_of(z[:, 0, :], 64), in1=heads_of(z[:, 1, :], 64), op=ALU.add)

        def rope(tt, rot, y_rot, add_eng, both=True):
            rope_sum(rope_products(tt, rot, both), y_rot, add_eng)

        xg_of = {}

        def turn_x(tp, sides=("A", "B")):
            xg = ilp.tile([P, 4096], BF16, name="xg", tag="il", align_bytes=64)
            xg_of[tp] = xg
            xg_words = xg[:].bitcast(F32).rearrange("p (a g r u) -> p a g r u", a=2, g=G, u=2)
            for a in range(2):
                tt = 2 * tp + a
                words = x_sb[tt][:].bitcast(F32)
                for gp in range(2):
                    xt = psum.tile([P, 512], F32, name="xt", tag=sides[gp])
                    for gl in range(2):
                        g = 2 * gp + gl
                        for u in range(2):
                            nc.tensor.transpose(
                                xt[:, (2 * gl + u) * P : (2 * gl + u + 1) * P],
                                words[:, 256 * g + u : 256 * (g + 1) : 2],
                                ident[:],
                            )
                    copy_on(
                        "s",
                        xg_words[:, a, 2 * gp : 2 * gp + 2, :, :],
                        xt[:].rearrange("p (g u r) -> p g r u", g=2, u=2),
                    )

        xt_of = {}

        def turn_x_pe(tp, sides=("A", "B")):
            for a in range(2):
                tt = 2 * tp + a
                words = x_sb[tt][:].bitcast(F32)
                for gp in range(2):
                    xt = psum.tile([P, 512], F32, name="xt", tag=sides[gp])
                    xt_of[(tt, gp)] = xt
                    for gl in range(2):
                        g = 2 * gp + gl
                        for u in range(2):
                            nc.tensor.transpose(
                                xt[:, (2 * gl + u) * P : (2 * gl + u + 1) * P],
                                words[:, 256 * g + u : 256 * (g + 1) : 2],
                                ident[:],
                            )

        def turn_x_out(tp):
            xg = ilp.tile([P, 4096], BF16, name="xg", tag="il", align_bytes=64)
            xg_of[tp] = xg
            xg_words = xg[:].bitcast(F32).rearrange("p (a g r u) -> p a g r u", a=2, g=G, u=2)
            for a in range(2):
                for gp in range(2):
                    copy_on(
                        "s",
                        xg_words[:, a, 2 * gp : 2 * gp + 2, :, :],
                        xt_of[(2 * tp + a, gp)][:].rearrange("p (g u r) -> p g r u", g=2, u=2),
                    )

        def quant_x(tp):
            nc.vector.quantize_mx(out=xc[tp][:].bitcast(FP8X4), scales=xs[tp][:], in_=xg_of[tp][:])

        vcs = {}

        def quant_v(gp, il):
            if "c" not in vcs:
                vcs["c"] = keep.tile([P, G, 512], U32, name="vc", tag="kvc", align_bytes=256)
                vcs["s"] = keep.tile([P, G, 512], U8, name="vs", tag="kvs", align_bytes=256)
            nc.vector.quantize_mx(
                out=vcs["c"][:, 2 * gp : 2 * gp + 2, :].rearrange("p g n -> p (g n)").bitcast(FP8X4),
                scales=vcs["s"][:, 2 * gp : 2 * gp + 2, :].rearrange("p g n -> p (g n)"),
                in_=il[:],
            )

        widen(0, 0, (1, 3), "v")
        widen(0, 0, (0, 2), "s")
        widen(0, 1, (1, 3), "v")
        widen(0, 1, (0, 2), "s")
        banks_q00 = fill_qc(0, 0, 0, ("A", "B"))
        make_tables()
        il_q(0, 0, ROT, "v", 4, 8)
        il_q(0, 0, PLAIN, "v", 4, 8)
        empty_qc(0, 0, 0, banks_q00[0])
        empty_qc(0, 0, 1, banks_q00[1])
        widen(0, 2, (0, 1, 3), "v")
        widen(0, 2, (2,), "s")
        il_q(0, 1, ROT, "v")
        il_q(0, 1, PLAIN, "v")
        quant_q(0, 0)
        turn_x(0)
        banks_k1 = fill_kg(1, "A")
        il_k(0)
        load_v(0)
        load_v(1)
        for j, g in ((1, 0), (1, 1)):
            load_q(j, g, 0, 2)
            load_q(j, g, 2, 2)
        widen(0, 3, (0, 1))
        empty_kg(1, banks_k1)
        quant_q(0, 1)
        quant_x(0)
        banks_k2 = fill_kg(2, "B")
        il_q(0, 2, ROT, "v")
        il_q(0, 2, PLAIN, "v")
        quant_k(0)
        widen(0, 3, (2, 3))
        quant_q(0, 2)
        banks_k3 = fill_kg(3, "A")
        empty_kg(2, banks_k2)
        empty_kg(3, banks_k3)
        load_v(2)
        load_v(3)
        for g in (2, 3):
            load_q(1, g, 0, 2)
            load_q(1, g, 2, 2)
        turn_x(1)
        quant_k(1)
        banks_v0 = fill_vg(0, "B")
        k_acc = banks_of("A")
        for tt in range(2):
            for g in range(G):
                one_pass(k_acc[tt][:], tt, g, kc[:, :, :], ks[:, :, :])
        il_q(0, 3, ROT, "v")
        quant_x(1)
        widen(1, 0)
        for tt in range(2, TT):
            for g in range(G):
                one_pass(k_acc[tt][:], tt, g, kc[:, :, :], ks[:, :, :])
        empty_vg(0, banks_v0)
        banks_v0b = fill_vg(1, "B")
        il_q(0, 3, PLAIN, "v")
        widen(1, 1, (0, 1))
        empty_vg(1, banks_v0b)
        il_v0 = ilv_of[0]
        banks_v2 = fill_vg(2, "B")
        bank_v3 = psum.tile([P, 1024], BF16, name="rt", tag="B")
        for k in range(2):
            nc.tensor.matmul(
                out=bank_v3[:].rearrange("p (c t) -> p t c", t=PACK)[:, 2 * k : 2 * k + 2, :],
                lhsT=ident_b[:],
                rhs=wv_raw[3][:, 2 * k : 2 * k + 2, 256:512],
                start=True,
                stop=True,
            )
        widen(1, 1, (2, 3))
        il_v3("v", 0, 256)

        y_k = {}
        for tt in range(TT):
            y_k[tt] = xy.tile([P, 512], F32, name="y_k", tag="xy")
            rope(tt, heads_of(k_acc[tt][:], 128)[:, :, 0:64], heads_of(y_k[tt][:], 128)[:, :, 0:64], nc.gpsimd, False)
        for tt in range(TT):
            copy_on("v" if tt < 2 else "s", heads_of(y_k[tt][:], 128)[:, :, 64:128], heads_of(k_acc[tt][:], 128)[:, :, 64:128])
            nc.sync.dma_start(out=k_out[tt * P : (tt + 1) * P, :], in_=y_k[tt][:])

        empty_vg(2, banks_v2)
        il_v1 = ilv_of[1]
        copy_on("s", ilv_of[1][:, 3072:4096].bitcast(F32), bank_v3[:].bitcast(F32))
        quant_q(0, 3)
        il_q(1, 0, ROT, "v")
        il_q(1, 0, PLAIN, "v")
        widen(1, 2)
        q_r = banks_of("A")
        passes(q_r, *q_half(0, ROT))
        q_p = banks_of("B")
        passes(q_p, *q_half(0, PLAIN))
        quant_v(0, il_v0)
        quant_q(1, 0)
        widen(1, 3)
        il_q(1, 1, ROT, "v")
        il_q(1, 1, PLAIN, "v")
        quant_v(1, il_v1)
        quant_q(1, 1)

        y_q = {}
        for tt in range(TT):
            y_q[tt] = xy.tile([P, 1024], F32, name="y_q", tag="xy")
            if tt < TT - 1:
                rope(tt, heads_of(q_r[tt][:], 64), heads_of(y_q[tt][:], 128)[:, :, 0:64], nc.gpsimd)
            else:
                z_last = rope_products(tt, heads_of(q_r[tt][:], 64))
        for tt in range(2):
            copy_on("v", heads_of(y_q[tt][:], 128)[:, :, 64:128], heads_of(q_p[tt][:], 64))
            nc.sync.dma_start(out=q_out[tt * P : (tt + 1) * P, 0:1024], in_=y_q[tt][:])
        rope_sum(z_last, heads_of(y_q[TT - 1][:], 128)[:, :, 0:64], nc.vector)
        for tt in range(2, TT):
            copy_on("s", heads_of(y_q[tt][:], 128)[:, :, 64:128], heads_of(q_p[tt][:], 64))
            nc.sync.dma_start(out=q_out[tt * P : (tt + 1) * P, 0:1024], in_=y_q[tt][:])

        v_acc = banks_of("A")
        passes(v_acc, vcs["c"][:, :, :], vcs["s"][:, :, :])
        rot_acc = banks_of("B")
        passes(rot_acc, *q_half(1, ROT), gs=(0, 1))

        il_q(1, 2, ROT, "v")
        il_q(1, 2, PLAIN, "s")
        il_q(1, 3, ROT, "v")
        il_q(1, 3, PLAIN, "s", 0, 6)
        quant_q(1, 2, (ROT,))
        passes(rot_acc, *q_half(1, ROT), gs=(2,))
        quant_q(1, 3, (ROT,))
        passes(rot_acc, *q_half(1, ROT), gs=(3,))
        il_q(1, 3, PLAIN, "v", 6, 8)
        quant_q(1, 2, (PLAIN,))
        quant_q(1, 3, (PLAIN,))
        plain_acc = {}
        for tt in range(TT):
            y = xy.tile([P, 512], F32, name="y_v", tag="y_v", bufs=4)
            copy_on("s", y[:], v_acc[tt][:])
            nc.sync.dma_start(out=v_out[tt * P : (tt + 1) * P, :], in_=y[:])
        for tt in range(TT):
            plain_acc[tt] = psum.tile([P, 512], F32, name="acc", tag="A")
            for g in range(G):
                one_pass(plain_acc[tt][:], tt, g, *q_half(1, PLAIN))

        for tt in range(TT):
            y_q[tt] = xy.tile([P, 1024], F32, name="y_q", tag="xy")
            copy_on("s", heads_of(y_q[tt][:], 128)[:, :, 64:128], heads_of(plain_acc[tt][:], 64))
            rot = heads_of(rot_acc[tt][:], 64)
            y_rot = heads_of(y_q[tt][:], 128)[:, :, 0:64]
            if tt < TT - 1:
                rope(tt, rot, y_rot, nc.gpsimd)
                nc.sync.dma_start(out=q_out[tt * P : (tt + 1) * P, 1024:2048], in_=y_q[tt][:])
            else:
                z_lo = rope_products(tt, rot[:, 0:4, :])
                z_hi = rope_products(tt, rot[:, 4:8, :])
                rope_sum(z_lo, y_rot[:, 0:4, :], nc.vector)
                nc.sync.dma_start(out=q_out[tt * P : (tt + 1) * P, 1024:1536], in_=y_q[tt][:, 0:512])
                rope_sum(z_hi, y_rot[:, 4:8, :], nc.vector)
                nc.sync.dma_start(out=q_out[tt * P : (tt + 1) * P, 1536:2048], in_=y_q[tt][:, 512:1024])
